import numpy as np
import ml_dtypes


def mxq(x, axis, fmt="e4m3"):
    dtype, down = {"e4m3": (ml_dtypes.float8_e4m3fn, 7), "e5m2": (ml_dtypes.float8_e5m2, 14)}[fmt]
    v = np.moveaxis(np.asarray(x, np.float32).astype(ml_dtypes.bfloat16).astype(np.float64), axis, -1)
    blocks = v.reshape(v.shape[:-1] + (-1, 32))
    amax = np.abs(blocks).max(-1, keepdims=True)
    byte = np.maximum(np.where(amax > 0, np.frexp(amax)[1] - 1 + 127, 0) - down, 1)
    scale = np.exp2(byte - 127.0)
    codes = (blocks / scale).astype(np.float32).astype(dtype).astype(np.float64)
    return np.moveaxis((codes * scale).reshape(v.shape), -1, axis)


WIDE = False


def mx_kscale(k):
    if not WIDE:
        return np.ones(k)
    levels = np.array([10, -10, 5, -5, 0])
    a = np.random.permutation(np.resize(levels, k // 512 * 4)).reshape(k // 512, 4)
    idx = np.arange(k)
    return np.exp2(a[idx // 512, idx % 128 // 32])


BF16 = ml_dtypes.bfloat16


def bf(x):
    return np.asarray(x, np.float32).astype(BF16)


def f64(x):
    return np.asarray(x).astype(np.float64)


B, T, D, H, E, C = 8, 1024, 1024, 8, 512, 512
HD = D // H
EPS = 1e-5


def setup_inputs():
    s = mx_kscale(D)
    fall = 0.35 / np.sqrt(1.0 + np.arange(T))
    return {"ret": bf(np.random.standard_normal((B, T, H, HD)) * fall[None, :, None, None]),
            "gamma": bf((1.0 + 0.1 * np.random.standard_normal(D)) * s),
            "beta": bf(0.1 * np.random.standard_normal(D) * s),
            "Wo": bf(np.random.standard_normal((D, E)) / np.sqrt(D) / s[:, None]),
            "bo": bf(0.1 * np.random.standard_normal(E))}


def reference(ret, gamma, beta, Wo, bo):
    r = f64(ret)
    mu = r.mean(-1, keepdims=True)
    var = r.var(-1, keepdims=True)
    z = (r - mu) / np.sqrt(var + EPS)
    y = z.reshape(B, T, D) * f64(gamma) + f64(beta)
    return (mxq(y, 2, "e4m3") @ mxq(f64(Wo), 0, "e4m3")) + f64(bo)

@@ -1,0 +1,232 @@
+from contextlib import ExitStack
+
+import concourse.mybir as mybir
+from concourse.masks import make_identity
+
+F32 = mybir.dt.float32
+BF16 = mybir.dt.bfloat16
+U32 = mybir.dt.uint32
+U8 = mybir.dt.uint8
+FP8X4 = mybir.dt.float8_e4m3fn_x4
+ACT = mybir.ActivationFunctionType
+ALU = mybir.AluOpType
+
+P = 128
+PACK = 4
+TOKENS = 8 * 1024
+HEADS = 8
+CH = 128
+D = HEADS * CH
+E = 512
+EPS = 1e-5
+PASSES = D // (P * PACK)
+TILES = 4
+GROUP = TILES * P
+N_GROUPS = TOKENS // GROUP
+ROWS = TILES * HEADS
+RUN = 4
+LOADS_AHEAD = 3
+
+FLOPS = 2 * TOKENS * D * E
+
+
+def tile_retentivenetwork_pb_t_kernel(tc, ret, gamma, beta, Wo, bo, out):
+    nc = tc.nc
+    ret_rows = ret.rearrange("b t h c -> (b t) (h c)")
+    out_rows = out.rearrange("b t e -> (b t) e")
+
+    with ExitStack() as ctx:
+        const = ctx.enter_context(tc.tile_pool(name="const", bufs=1))
+        r_pool = ctx.enter_context(tc.tile_pool(name="r", bufs=LOADS_AHEAD + 1))
+        stat_pool = ctx.enter_context(tc.tile_pool(name="stat", bufs=3))
+        z_pool = ctx.enter_context(tc.tile_pool(name="z", bufs=2))
+        y_pool = ctx.enter_context(tc.tile_pool(name="y", bufs=2))
+        q_pool = ctx.enter_context(tc.tile_pool(name="q", bufs=2))
+        o_pool = ctx.enter_context(tc.tile_pool(name="o", bufs=2))
+        psum_t = ctx.enter_context(tc.psum_pool(name="psum_t", bufs=4))
+        psum_o = ctx.enter_context(tc.psum_pool(name="psum_o", bufs=4))
+
+        r_of, sums_of, std_of, rstd_of, shift_of, z_of, y_of = {}, {}, {}, {}, {}, {}, {}
+        codes_of, scales_of, acc_of = {}, {}, {}
+
+        def load(i):
+            r = r_pool.tile([P, TILES, D], BF16)
+            rows = ret_rows[i * GROUP : (i + 1) * GROUP, :]
+            nc.sync.dma_start(out=r[:], in_=rows.rearrange("(p j) k -> p j k", j=TILES))
+            r_of[i] = r
+
+        load(0)
+        w_raw = const.tile([P, PASSES * PACK, E], BF16)
+        nc.sync.dma_start(out=w_raw[:], in_=Wo.rearrange("(s p) n -> p s n", p=P))
+        for i in range(1, LOADS_AHEAD):
+            load(i)
+
+        ident = const.tile([P, P], F32)
+        make_identity(nc, ident[:])
+
+        gb_rows = const.tile([P, P], BF16)
+        nc.vector.memset(gb_rows[:], 0.0)
+        nc.scalar.dma_start(out=gb_rows[0:HEADS, :], in_=gamma.rearrange("(h c) -> h c", c=CH))
+        nc.scalar.dma_start(out=gb_rows[HEADS : 2 * HEADS, :], in_=beta.rearrange("(h c) -> h c", c=CH))
+        bo_all = const.tile([P, E], BF16)
+        nc.scalar.dma_start(out=bo_all[:], in_=bo.partition_broadcast(P))
+        gb_f32 = const.tile([P, P], F32)
+        nc.vector.tensor_copy(out=gb_f32[:], in_=gb_rows[:])
+        gb_t = psum_t.tile([P, GROUP], F32, tag="zt")
+        nc.tensor.transpose(gb_t[:, 0:P], gb_f32[:], ident[:])
+        gb_col = const.tile([P, 2 * HEADS], F32)
+        nc.vector.tensor_copy(out=gb_col[:], in_=gb_t[:, 0 : 2 * HEADS])
+
+        w_codes = const.tile([P, PASSES, E], U32, align_bytes=64)
+        w_scales = const.tile([P, PASSES, E], U8, align_bytes=64)
+
+        def regroup(dst, src):
+            nc.vector.tensor_copy(
+                out=dst.rearrange("p (c i) t -> p c t i", i=RUN),
+                in_=src.rearrange("p t (c i) -> p c t i", i=RUN),
+            )
+
+        def quantise_weights():
+            for g in range(PASSES):
+                w_grouped = const.tile([P, E, PACK], BF16, align_bytes=64, tag="w_grouped%d" % g)
+                regroup(w_grouped[:], w_raw[:, g * PACK : (g + 1) * PACK, :])
+                nc.vector.quantize_mx(
+                    out=w_codes[:, g, :].bitcast(FP8X4),
+                    scales=w_scales[:, g, :],
+                    in_=w_grouped[:].rearrange("p w t -> p (w t)"),
+                )
+
+        def moments(i):
+            r = r_of[i]
+            st = stat_pool.tile([P, ROWS, 6], F32)
+            for j in range(TILES):
+                for h in range(HEADS):
+                    nc.vector.bn_stats(out=st[:, j * HEADS + h, :], in_=r[:, j, h * CH : (h + 1) * CH])
+            mean_even, m2_even = st[:, :, 1], st[:, :, 2]
+            mean_odd, m2_odd = st[:, :, 4], st[:, :, 5]
+            diff = stat_pool.tile([P, ROWS], F32)
+            m2 = stat_pool.tile([P, ROWS], F32)
+            mean2 = stat_pool.tile([P, ROWS], F32)
+            between = stat_pool.tile([P, ROWS], F32)
+            var128 = stat_pool.tile([P, ROWS], F32)
+            nc.vector.tensor_tensor(out=diff[:], in0=mean_even, in1=mean_odd, op=ALU.subtract)
+            nc.vector.scalar_tensor_tensor(
+                out=m2[:], in0=m2_even, scalar=CH * EPS, in1=m2_odd, op0=ALU.add, op1=ALU.add
+            )
+            nc.vector.tensor_tensor(out=mean2[:], in0=mean_even, in1=mean_odd, op=ALU.add)
+            nc.vector.scalar_tensor_tensor(
+                out=between[:], in0=diff[:], scalar=CH / 4.0, in1=diff[:], op0=ALU.mult, op1=ALU.mult
+            )
+            nc.vector.tensor_tensor(out=var128[:], in0=between[:], in1=m2[:], op=ALU.add)
+            sums_of[i] = (mean2, var128)
+
+        def deviation(i):
+            std = stat_pool.tile([P, ROWS], F32)
+            nc.scalar.activation(out=std[:], in_=sums_of[i][1][:], func=ACT.Sqrt, scale=1.0 / CH)
+            std_of[i] = std
+
+        def scale_and_shift(i):
+            rstd = stat_pool.tile([P, ROWS], F32)
+            shift = stat_pool.tile([P, ROWS], F32)
+            nc.vector.reciprocal(out=rstd[:], in_=std_of[i][:])
+            nc.vector.scalar_tensor_tensor(
+                out=shift[:], in0=sums_of[i][0][:], scalar=-0.5, in1=rstd[:], op0=ALU.mult, op1=ALU.mult
+            )
+            rstd_of[i] = rstd
+            shift_of[i] = shift
+
+        def normalise(i):
+            r, rstd, shift = r_of[i], rstd_of[i], shift_of[i]
+            z = z_pool.tile([P, TILES, D], F32)
+            for h in range(HEADS):
+                for j in range(TILES):
+                    row = j * HEADS + h
+                    nc.scalar.activation(
+                        out=z[:, j, h * CH : (h + 1) * CH],
+                        in_=r[:, j, h * CH : (h + 1) * CH],
+                        func=ACT.Identity,
+                        scale=rstd[:, row : row + 1],
+                        bias=shift[:, row : row + 1],
+                    )
+            z_of[i] = z
+
+        def transpose_and_affine(i):
+            z = z_of[i]
+            y = y_pool.tile([P, HEADS, GROUP], BF16)
+            for h in range(HEADS):
+                zt = psum_t.tile([P, GROUP], F32)
+                for j in range(TILES):
+                    nc.tensor.transpose(zt[:, j * P : (j + 1) * P], z[:, j, h * CH : (h + 1) * CH], ident[:])
+                nc.scalar.activation(
+                    out=y[:, h, :],
+                    in_=zt[:],
+                    func=ACT.Identity,
+                    scale=gb_col[:, h : h + 1],
+                    bias=gb_col[:, HEADS + h : HEADS + h + 1],
+                )
+            y_of[i] = y
+
+        def quantise(i, g):
+            if g == 0:
+                codes = q_pool.tile([P, PASSES, GROUP], U32, align_bytes=64)
+                scales = q_pool.tile([P, PASSES, GROUP], U8, align_bytes=64)
+                codes_of[i] = codes
+                scales_of[i] = scales
+            grouped = q_pool.tile([P, GROUP, PACK], BF16, align_bytes=64)
+            regroup(grouped[:], y_of[i][:, g * PACK : (g + 1) * PACK, :])
+            nc.vector.quantize_mx(
+                out=codes_of[i][:, g, :].bitcast(FP8X4),
+                scales=scales_of[i][:, g, :],
+                in_=grouped[:].rearrange("p w t -> p (w t)"),
+            )
+
+        def project(i):
+            codes, scales = codes_of[i], scales_of[i]
+            accs = []
+            for j in range(TILES):
+                acc = psum_o.tile([P, E], F32)
+                for g in range(PASSES):
+                    nc.tensor.matmul_mx(
+                        out=acc[:],
+                        lhsT=codes[:, g, j * P : (j + 1) * P].bitcast(FP8X4),
+                        lhsT_scale=scales[:, g, j * P : (j + 1) * P],
+                        rhs=w_codes[:, g, :].bitcast(FP8X4),
+                        rhs_scale=w_scales[:, g, :],
+                        start=(g == 0),
+                        stop=(g == PASSES - 1),
+                    )
+                accs.append(acc)
+            acc_of[i] = accs
+
+        def add_bias_and_store(i):
+            o = o_pool.tile([P, TILES, E], F32)
+            for j in range(TILES):
+                nc.vector.tensor_tensor(out=o[:, j, :], in0=acc_of[i][j][:], in1=bo_all[:], op=ALU.add)
+            rows = out_rows[i * GROUP : (i + 1) * GROUP, :]
+            nc.sync.dma_start(out=rows.rearrange("(p j) e -> p j e", j=TILES), in_=o[:])
+
+        def exists(i):
+            return 0 <= i < N_GROUPS
+
+        for i in range(-1, N_GROUPS + 2):
+            if i >= 0 and exists(i + LOADS_AHEAD):
+                load(i + LOADS_AHEAD)
+            if exists(i + 1):
+                moments(i + 1)
+            if exists(i):
+                normalise(i)
+            if exists(i + 1):
+                deviation(i + 1)
+            if exists(i - 2):
+                add_bias_and_store(i - 2)
+            if exists(i):
+                transpose_and_affine(i)
+            if exists(i - 1):
+                quantise(i - 1, 0)
+            if exists(i + 1):
+                scale_and_shift(i + 1)
+            if i == -1:
+                quantise_weights()
+            if exists(i - 1):
+                quantise(i - 1, 1)
+                project(i - 1)

@@ -51,8 +51,12 @@ def tile_retentivenetwork_pb_t_kernel(tc, ret, gamma, beta, Wo, bo, out):
 
         def load(i):
             r = r_pool.tile([P, TILES, D], BF16)
-            rows = ret_rows[i * GROUP : (i + 1) * GROUP, :]
-            nc.sync.dma_start(out=r[:], in_=rows.rearrange("(p j) k -> p j k", j=TILES))
+            rows = ret_rows[i * GROUP : (i + 1) * GROUP, :].rearrange("(p j) k -> p j k", j=TILES)
+            if i == 0:
+                for j in range(TILES):
+                    nc.sync.dma_start(out=r[:, j, :], in_=rows[:, j, :])
+            else:
+                nc.sync.dma_start(out=r[:], in_=rows)
             r_of[i] = r
 
         load(0)
@@ -63,6 +67,10 @@ def tile_retentivenetwork_pb_t_kernel(tc, ret, gamma, beta, Wo, bo, out):
 
         ident = const.tile([P, P], F32)
         make_identity(nc, ident[:])
+
+        one = const.tile([P, 1], F32)
+        nc.vector.memset(one[:], 1.0)
+        nc.scalar.activation(out=one[:], in_=one[:], func=ACT.Sqrt)
 
         gb_rows = const.tile([P, P], BF16)
         nc.vector.memset(gb_rows[:], 0.0)
@@ -107,17 +115,17 @@ def tile_retentivenetwork_pb_t_kernel(tc, ret, gamma, beta, Wo, bo, out):
             diff = stat_pool.tile([P, ROWS], F32)
             m2 = stat_pool.tile([P, ROWS], F32)
             mean2 = stat_pool.tile([P, ROWS], F32)
+            square = stat_pool.tile([P, ROWS], F32)
             between = stat_pool.tile([P, ROWS], F32)
             var128 = stat_pool.tile([P, ROWS], F32)
-            nc.vector.tensor_tensor(out=diff[:], in0=mean_even, in1=mean_odd, op=ALU.subtract)
-            nc.vector.scalar_tensor_tensor(
-                out=m2[:], in0=m2_even, scalar=CH * EPS, in1=m2_odd, op0=ALU.add, op1=ALU.add
+            nc.gpsimd.tensor_tensor(out=diff[:], in0=mean_even, in1=mean_odd, op=ALU.subtract)
+            nc.gpsimd.tensor_tensor(out=m2[:], in0=m2_even, in1=m2_odd, op=ALU.add)
+            nc.gpsimd.tensor_tensor(out=square[:], in0=diff[:], in1=diff[:], op=ALU.mult)
+            nc.gpsimd.tensor_tensor(out=mean2[:], in0=mean_even, in1=mean_odd, op=ALU.add)
+            nc.gpsimd.tensor_scalar(
+                out=between[:], in0=square[:], scalar1=CH / 4.0, scalar2=CH * EPS, op0=ALU.mult, op1=ALU.add
             )
-            nc.vector.tensor_tensor(out=mean2[:], in0=mean_even, in1=mean_odd, op=ALU.add)
-            nc.vector.scalar_tensor_tensor(
-                out=between[:], in0=diff[:], scalar=CH / 4.0, in1=diff[:], op0=ALU.mult, op1=ALU.mult
-            )
-            nc.vector.tensor_tensor(out=var128[:], in0=between[:], in1=m2[:], op=ALU.add)
+            nc.gpsimd.tensor_tensor(out=var128[:], in0=between[:], in1=m2[:], op=ALU.add)
             sums_of[i] = (mean2, var128)
 
         def deviation(i):
@@ -150,10 +158,13 @@ def tile_retentivenetwork_pb_t_kernel(tc, ret, gamma, beta, Wo, bo, out):
                     )
             z_of[i] = z
 
-        def transpose_and_affine(i):
+        def transpose_and_affine(i, g):
             z = z_of[i]
-            y = y_pool.tile([P, HEADS, GROUP], BF16)
-            for h in range(HEADS):
+            if g == 0:
+                y = y_pool.tile([P, HEADS, GROUP], BF16)
+                y_of[i] = y
+            y = y_of[i]
+            for h in range(g * PACK, (g + 1) * PACK):
                 zt = psum_t.tile([P, GROUP], F32)
                 for j in range(TILES):
                     nc.tensor.transpose(zt[:, j * P : (j + 1) * P], z[:, j, h * CH : (h + 1) * CH], ident[:])
@@ -164,7 +175,6 @@ def tile_retentivenetwork_pb_t_kernel(tc, ret, gamma, beta, Wo, bo, out):
                     scale=gb_col[:, h : h + 1],
                     bias=gb_col[:, HEADS + h : HEADS + h + 1],
                 )
-            y_of[i] = y
 
         def quantise(i, g):
             if g == 0:
@@ -215,12 +225,14 @@ def tile_retentivenetwork_pb_t_kernel(tc, ret, gamma, beta, Wo, bo, out):
                 moments(i + 1)
             if exists(i):
                 normalise(i)
-            if exists(i + 1):
-                deviation(i + 1)
             if exists(i - 2):
                 add_bias_and_store(i - 2)
             if exists(i):
-                transpose_and_affine(i)
+                transpose_and_affine(i, 0)
+            if exists(i + 1):
+                deviation(i + 1)
+            if exists(i):
+                transpose_and_affine(i, 1)
             if exists(i - 1):
                 quantise(i - 1, 0)
             if exists(i + 1):

@@ -25,7 +25,8 @@ GROUP = TILES * P
 N_GROUPS = TOKENS // GROUP
 ROWS = TILES * HEADS
 RUN = 4
-LOADS_AHEAD = 3
+BANKS_T = 4
+LOADS_AHEAD = 4
 
 FLOPS = 2 * TOKENS * D * E
 
@@ -40,14 +41,15 @@ def tile_retentivenetwork_pb_t_kernel(tc, ret, gamma, beta, Wo, bo, out):
         r_pool = ctx.enter_context(tc.tile_pool(name="r", bufs=LOADS_AHEAD + 1))
         stat_pool = ctx.enter_context(tc.tile_pool(name="stat", bufs=3))
         z_pool = ctx.enter_context(tc.tile_pool(name="z", bufs=2))
-        y_pool = ctx.enter_context(tc.tile_pool(name="y", bufs=2))
+        y_pool = ctx.enter_context(tc.tile_pool(name="y", bufs=3))
         q_pool = ctx.enter_context(tc.tile_pool(name="q", bufs=2))
         o_pool = ctx.enter_context(tc.tile_pool(name="o", bufs=2))
-        psum_t = ctx.enter_context(tc.psum_pool(name="psum_t", bufs=4))
-        psum_o = ctx.enter_context(tc.psum_pool(name="psum_o", bufs=4))
+        psum_t = ctx.enter_context(tc.psum_pool(name="psum_t", bufs=BANKS_T))
+        psum_o = ctx.enter_context(tc.psum_pool(name="psum_o", bufs=TILES))
+        ctx.enter_context(tc.manual_schedule())
 
-        r_of, sums_of, std_of, rstd_of, shift_of, z_of, y_of = {}, {}, {}, {}, {}, {}, {}
-        codes_of, scales_of, acc_of = {}, {}, {}
+        r_of, st_of, minus_mean_of, var128_of, std_of, rstd_of, shift_of = {}, {}, {}, {}, {}, {}, {}
+        z_of, zt_of, y_of, grouped_of, codes_of, scales_of, acc_of = {}, {}, {}, {}, {}, {}, {}
 
         def load(i):
             r = r_pool.tile([P, TILES, D], BF16)
@@ -60,17 +62,12 @@ def tile_retentivenetwork_pb_t_kernel(tc, ret, gamma, beta, Wo, bo, out):
             r_of[i] = r
 
         load(0)
+        load(1)
         w_raw = const.tile([P, PASSES * PACK, E], BF16)
         nc.sync.dma_start(out=w_raw[:], in_=Wo.rearrange("(s p) n -> p s n", p=P))
-        for i in range(1, LOADS_AHEAD):
-            load(i)
 
         ident = const.tile([P, P], F32)
         make_identity(nc, ident[:])
-
-        one = const.tile([P, 1], F32)
-        nc.vector.memset(one[:], 1.0)
-        nc.scalar.activation(out=one[:], in_=one[:], func=ACT.Sqrt)
 
         gb_rows = const.tile([P, P], BF16)
         nc.vector.memset(gb_rows[:], 0.0)
@@ -78,12 +75,19 @@ def tile_retentivenetwork_pb_t_kernel(tc, ret, gamma, beta, Wo, bo, out):
         nc.scalar.dma_start(out=gb_rows[HEADS : 2 * HEADS, :], in_=beta.rearrange("(h c) -> h c", c=CH))
         bo_all = const.tile([P, E], BF16)
         nc.scalar.dma_start(out=bo_all[:], in_=bo.partition_broadcast(P))
-        gb_f32 = const.tile([P, P], F32)
-        nc.vector.tensor_copy(out=gb_f32[:], in_=gb_rows[:])
-        gb_t = psum_t.tile([P, GROUP], F32, tag="zt")
-        nc.tensor.transpose(gb_t[:, 0:P], gb_f32[:], ident[:])
+
+        one = const.tile([P, 1], F32)
+        nc.vector.memset(one[:], 1.0)
+        nc.scalar.activation(out=one[:], in_=one[:], func=ACT.Sqrt)
+
         gb_col = const.tile([P, 2 * HEADS], F32)
-        nc.vector.tensor_copy(out=gb_col[:], in_=gb_t[:, 0 : 2 * HEADS])
+
+        def gamma_beta_to_partitions():
+            gb_f32 = const.tile([P, P], F32)
+            nc.vector.tensor_copy(out=gb_f32[:], in_=gb_rows[:])
+            gb_t = psum_t.tile([P, GROUP], F32, tag="zt")
+            nc.tensor.transpose(gb_t[:, 0:P], gb_f32[:], ident[:])
+            nc.vector.tensor_copy(out=gb_col[:], in_=gb_t[:, 0 : 2 * HEADS])
 
         w_codes = const.tile([P, PASSES, E], U32, align_bytes=64)
         w_scales = const.tile([P, PASSES, E], U8, align_bytes=64)
@@ -104,77 +108,92 @@ def tile_retentivenetwork_pb_t_kernel(tc, ret, gamma, beta, Wo, bo, out):
                     in_=w_grouped[:].rearrange("p w t -> p (w t)"),
                 )
 
-        def moments(i):
-            r = r_of[i]
-            st = stat_pool.tile([P, ROWS, 6], F32)
-            for j in range(TILES):
+        def halves(i, tiles):
+            if tiles[0] == 0:
+                st = stat_pool.tile([P, ROWS, 6], F32)
+                st_of[i] = st
+            for j in tiles:
                 for h in range(HEADS):
-                    nc.vector.bn_stats(out=st[:, j * HEADS + h, :], in_=r[:, j, h * CH : (h + 1) * CH])
+                    nc.vector.bn_stats(
+                        out=st_of[i][:, j * HEADS + h, :], in_=r_of[i][:, j, h * CH : (h + 1) * CH]
+                    )
+
+        def join_halves(i):
+            st = st_of[i]
             mean_even, m2_even = st[:, :, 1], st[:, :, 2]
             mean_odd, m2_odd = st[:, :, 4], st[:, :, 5]
             diff = stat_pool.tile([P, ROWS], F32)
             m2 = stat_pool.tile([P, ROWS], F32)
             mean2 = stat_pool.tile([P, ROWS], F32)
+            minus_mean = stat_pool.tile([P, ROWS], F32)
             square = stat_pool.tile([P, ROWS], F32)
             between = stat_pool.tile([P, ROWS], F32)
             var128 = stat_pool.tile([P, ROWS], F32)
             nc.gpsimd.tensor_tensor(out=diff[:], in0=mean_even, in1=mean_odd, op=ALU.subtract)
             nc.gpsimd.tensor_tensor(out=m2[:], in0=m2_even, in1=m2_odd, op=ALU.add)
             nc.gpsimd.tensor_tensor(out=square[:], in0=diff[:], in1=diff[:], op=ALU.mult)
-            nc.gpsimd.tensor_tensor(out=mean2[:], in0=mean_even, in1=mean_odd, op=ALU.add)
             nc.gpsimd.tensor_scalar(
                 out=between[:], in0=square[:], scalar1=CH / 4.0, scalar2=CH * EPS, op0=ALU.mult, op1=ALU.add
             )
             nc.gpsimd.tensor_tensor(out=var128[:], in0=between[:], in1=m2[:], op=ALU.add)
-            sums_of[i] = (mean2, var128)
+            nc.gpsimd.tensor_tensor(out=mean2[:], in0=mean_even, in1=mean_odd, op=ALU.add)
+            nc.gpsimd.tensor_scalar(
+                out=minus_mean[:], in0=mean2[:], scalar1=-0.5, scalar2=0.0, op0=ALU.mult, op1=ALU.add
+            )
+            minus_mean_of[i] = minus_mean
+            var128_of[i] = var128
 
         def deviation(i):
             std = stat_pool.tile([P, ROWS], F32)
-            nc.scalar.activation(out=std[:], in_=sums_of[i][1][:], func=ACT.Sqrt, scale=1.0 / CH)
+            nc.scalar.activation(out=std[:], in_=var128_of[i][:], func=ACT.Sqrt, scale=1.0 / CH)
             std_of[i] = std
 
-        def scale_and_shift(i):
+        def reciprocal(i):
             rstd = stat_pool.tile([P, ROWS], F32)
-            shift = stat_pool.tile([P, ROWS], F32)
             nc.vector.reciprocal(out=rstd[:], in_=std_of[i][:])
-            nc.vector.scalar_tensor_tensor(
-                out=shift[:], in0=sums_of[i][0][:], scalar=-0.5, in1=rstd[:], op0=ALU.mult, op1=ALU.mult
-            )
             rstd_of[i] = rstd
-            shift_of[i] = shift
 
-        def normalise(i):
-            r, rstd, shift = r_of[i], rstd_of[i], shift_of[i]
-            z = z_pool.tile([P, TILES, D], F32)
-            for h in range(HEADS):
-                for j in range(TILES):
-                    row = j * HEADS + h
-                    nc.scalar.activation(
-                        out=z[:, j, h * CH : (h + 1) * CH],
-                        in_=r[:, j, h * CH : (h + 1) * CH],
-                        func=ACT.Identity,
-                        scale=rstd[:, row : row + 1],
-                        bias=shift[:, row : row + 1],
-                    )
-            z_of[i] = z
+        def shift(i):
+            shift_tile = stat_pool.tile([P, ROWS], F32)
+            nc.gpsimd.tensor_tensor(out=shift_tile[:], in0=minus_mean_of[i][:], in1=rstd_of[i][:], op=ALU.mult)
+            shift_of[i] = shift_tile
 
-        def transpose_and_affine(i, g):
-            z = z_of[i]
-            if g == 0:
+        def normalise(i, h):
+            if h == 0:
+                z = z_pool.tile([P, TILES, D], F32)
+                z_of[i] = z
+            for j in range(TILES):
+                row = j * HEADS + h
+                nc.scalar.activation(
+                    out=z_of[i][:, j, h * CH : (h + 1) * CH],
+                    in_=r_of[i][:, j, h * CH : (h + 1) * CH],
+                    func=ACT.Identity,
+                    scale=rstd_of[i][:, row : row + 1],
+                    bias=shift_of[i][:, row : row + 1],
+                )
+
+        def transpose(i, h):
+            zt = psum_t.tile([P, GROUP], F32)
+            for j in range(TILES):
+                nc.tensor.transpose(zt[:, j * P : (j + 1) * P], z_of[i][:, j, h * CH : (h + 1) * CH], ident[:])
+            zt_of[(i, h)] = zt
+
+        def affine(i, h):
+            if h == 0:
                 y = y_pool.tile([P, HEADS, GROUP], BF16)
                 y_of[i] = y
-            y = y_of[i]
-            for h in range(g * PACK, (g + 1) * PACK):
-                zt = psum_t.tile([P, GROUP], F32)
-                for j in range(TILES):
-                    nc.tensor.transpose(zt[:, j * P : (j + 1) * P], z[:, j, h * CH : (h + 1) * CH], ident[:])
-                nc.scalar.activation(
-                    out=y[:, h, :],
-                    in_=zt[:],
-                    func=ACT.Identity,
-                    scale=gb_col[:, h : h + 1],
-                    bias=gb_col[:, HEADS + h : HEADS + h + 1],
-                )
+            nc.scalar.activation(
+                out=y_of[i][:, h, :],
+                in_=zt_of[(i, h)][:],
+                func=ACT.Identity,
+                scale=gb_col[:, h : h + 1],
+                bias=gb_col[:, HEADS + h : HEADS + h + 1],
+            )
+
+        def group_words(i, g):
+            grouped = q_pool.tile([P, GROUP, PACK], BF16, align_bytes=64)
+            regroup(grouped[:], y_of[i][:, g * PACK : (g + 1) * PACK, :])
+            grouped_of[(i, g)] = grouped
 
         def quantise(i, g):
             if g == 0:
@@ -182,12 +201,10 @@ def tile_retentivenetwork_pb_t_kernel(tc, ret, gamma, beta, Wo, bo, out):
                 scales = q_pool.tile([P, PASSES, GROUP], U8, align_bytes=64)
                 codes_of[i] = codes
                 scales_of[i] = scales
-            grouped = q_pool.tile([P, GROUP, PACK], BF16, align_bytes=64)
-            regroup(grouped[:], y_of[i][:, g * PACK : (g + 1) * PACK, :])
             nc.vector.quantize_mx(
                 out=codes_of[i][:, g, :].bitcast(FP8X4),
                 scales=scales_of[i][:, g, :],
-                in_=grouped[:].rearrange("p w t -> p (w t)"),
+                in_=grouped_of[(i, g)][:].rearrange("p w t -> p (w t)"),
             )
 
         def project(i):
@@ -195,9 +212,11 @@ def tile_retentivenetwork_pb_t_kernel(tc, ret, gamma, beta, Wo, bo, out):
             accs = []
             for j in range(TILES):
                 acc = psum_o.tile([P, E], F32)
-                for g in range(PASSES):
+                accs.append(acc)
+            for g in range(PASSES):
+                for j in range(TILES):
                     nc.tensor.matmul_mx(
-                        out=acc[:],
+                        out=accs[j][:],
                         lhsT=codes[:, g, j * P : (j + 1) * P].bitcast(FP8X4),
                         lhsT_scale=scales[:, g, j * P : (j + 1) * P],
                         rhs=w_codes[:, g, :].bitcast(FP8X4),
@@ -205,40 +224,54 @@ def tile_retentivenetwork_pb_t_kernel(tc, ret, gamma, beta, Wo, bo, out):
                         start=(g == 0),
                         stop=(g == PASSES - 1),
                     )
-                accs.append(acc)
             acc_of[i] = accs
 
         def add_bias_and_store(i):
             o = o_pool.tile([P, TILES, E], F32)
+            rows = out_rows[i * GROUP : (i + 1) * GROUP, :].rearrange("(p j) e -> p j e", j=TILES)
             for j in range(TILES):
                 nc.vector.tensor_tensor(out=o[:, j, :], in0=acc_of[i][j][:], in1=bo_all[:], op=ALU.add)
-            rows = out_rows[i * GROUP : (i + 1) * GROUP, :]
-            nc.sync.dma_start(out=rows.rearrange("(p j) e -> p j e", j=TILES), in_=o[:])
+                if i == N_GROUPS - 1:
+                    nc.sync.dma_start(out=rows[:, j, :], in_=o[:, j, :])
+            if i < N_GROUPS - 1:
+                nc.sync.dma_start(out=rows, in_=o[:])
 
         def exists(i):
             return 0 <= i < N_GROUPS
 
-        for i in range(-1, N_GROUPS + 2):
-            if i >= 0 and exists(i + LOADS_AHEAD):
+        for i in range(-2, N_GROUPS + 2):
+            if exists(i + LOADS_AHEAD):
                 load(i + LOADS_AHEAD)
+            if exists(i + 2):
+                halves(i + 2, range(0, TILES // 2))
             if exists(i + 1):
-                moments(i + 1)
+                reciprocal(i + 1)
+                shift(i + 1)
+            if exists(i + 2):
+                halves(i + 2, range(TILES // 2, TILES))
+                join_halves(i + 2)
+            if i == -1:
+                gamma_beta_to_partitions()
             if exists(i):
-                normalise(i)
+                for h in range(BANKS_T):
+                    affine(i, h)
+                    transpose(i, h + BANKS_T)
+                for h in range(BANKS_T, HEADS):
+                    affine(i, h)
+            if exists(i + 1):
+                for h in range(HEADS):
+                    normalise(i + 1, h)
+                    if h < BANKS_T:
+                        transpose(i + 1, h)
+            if exists(i + 2):
+                deviation(i + 2)
             if exists(i - 2):
                 add_bias_and_store(i - 2)
-            if exists(i):
-                transpose_and_affine(i, 0)
-            if exists(i + 1):
-                deviation(i + 1)
-            if exists(i):
-                transpose_and_affine(i, 1)
-            if exists(i - 1):
-                quantise(i - 1, 0)
-            if exists(i + 1):
-                scale_and_shift(i + 1)
-            if i == -1:
+            if i == 0:
                 quantise_weights()
             if exists(i - 1):
-                quantise(i - 1, 1)
+                for g in range(PASSES):
+                    group_words(i - 1, g)
+                for g in range(PASSES):
+                    quantise(i - 1, g)
                 project(i - 1)

@@ -48,7 +48,7 @@ def tile_retentivenetwork_pb_t_kernel(tc, ret, gamma, beta, Wo, bo, out):
         psum_o = ctx.enter_context(tc.psum_pool(name="psum_o", bufs=TILES))
         ctx.enter_context(tc.manual_schedule())
 
-        r_of, st_of, minus_mean_of, var128_of, std_of, rstd_of, shift_of = {}, {}, {}, {}, {}, {}, {}
+        r_of, st_of, minus_mean_of, var_eps_of, std_of, rstd_of, shift_of = {}, {}, {}, {}, {}, {}, {}
         z_of, zt_of, y_of, grouped_of, codes_of, scales_of, acc_of = {}, {}, {}, {}, {}, {}, {}
 
         def load(i):
@@ -108,44 +108,34 @@ def tile_retentivenetwork_pb_t_kernel(tc, ret, gamma, beta, Wo, bo, out):
                     in_=w_grouped[:].rearrange("p w t -> p (w t)"),
                 )
 
-        def halves(i, tiles):
+        def moments(i, tiles):
             if tiles[0] == 0:
-                st = stat_pool.tile([P, ROWS, 6], F32)
+                st = stat_pool.tile([P, ROWS, 3], F32)
                 st_of[i] = st
             for j in tiles:
-                for h in range(HEADS):
+                for pair in range(HEADS // 2):
+                    row = j * HEADS + 2 * pair
                     nc.vector.bn_stats(
-                        out=st_of[i][:, j * HEADS + h, :], in_=r_of[i][:, j, h * CH : (h + 1) * CH]
+                        out=st_of[i][:, row : row + 2, :].rearrange("p a s -> p (a s)"),
+                        in_=r_of[i][:, j, 2 * pair * CH : (2 * pair + 2) * CH].rearrange("p (a c) -> p c a", a=2),
                     )
 
-        def join_halves(i):
+        def variance(i):
             st = st_of[i]
-            mean_even, m2_even = st[:, :, 1], st[:, :, 2]
-            mean_odd, m2_odd = st[:, :, 4], st[:, :, 5]
-            diff = stat_pool.tile([P, ROWS], F32)
-            m2 = stat_pool.tile([P, ROWS], F32)
-            mean2 = stat_pool.tile([P, ROWS], F32)
+            var_eps = stat_pool.tile([P, ROWS], F32)
             minus_mean = stat_pool.tile([P, ROWS], F32)
-            square = stat_pool.tile([P, ROWS], F32)
-            between = stat_pool.tile([P, ROWS], F32)
-            var128 = stat_pool.tile([P, ROWS], F32)
-            nc.gpsimd.tensor_tensor(out=diff[:], in0=mean_even, in1=mean_odd, op=ALU.subtract)
-            nc.gpsimd.tensor_tensor(out=m2[:], in0=m2_even, in1=m2_odd, op=ALU.add)
-            nc.gpsimd.tensor_tensor(out=square[:], in0=diff[:], in1=diff[:], op=ALU.mult)
             nc.gpsimd.tensor_scalar(
-                out=between[:], in0=square[:], scalar1=CH / 4.0, scalar2=CH * EPS, op0=ALU.mult, op1=ALU.add
+                out=var_eps[:], in0=st[:, :, 2], scalar1=1.0 / CH, scalar2=EPS, op0=ALU.mult, op1=ALU.add
             )
-            nc.gpsimd.tensor_tensor(out=var128[:], in0=between[:], in1=m2[:], op=ALU.add)
-            nc.gpsimd.tensor_tensor(out=mean2[:], in0=mean_even, in1=mean_odd, op=ALU.add)
             nc.gpsimd.tensor_scalar(
-                out=minus_mean[:], in0=mean2[:], scalar1=-0.5, scalar2=0.0, op0=ALU.mult, op1=ALU.add
+                out=minus_mean[:], in0=st[:, :, 1], scalar1=-1.0, scalar2=0.0, op0=ALU.mult, op1=ALU.add
             )
+            var_eps_of[i] = var_eps
             minus_mean_of[i] = minus_mean
-            var128_of[i] = var128
 
         def deviation(i):
             std = stat_pool.tile([P, ROWS], F32)
-            nc.scalar.activation(out=std[:], in_=var128_of[i][:], func=ACT.Sqrt, scale=1.0 / CH)
+            nc.scalar.activation(out=std[:], in_=var_eps_of[i][:], func=ACT.Sqrt)
             std_of[i] = std
 
         def reciprocal(i):
@@ -164,13 +154,23 @@ def tile_retentivenetwork_pb_t_kernel(tc, ret, gamma, beta, Wo, bo, out):
                 z_of[i] = z
             for j in range(TILES):
                 row = j * HEADS + h
-                nc.scalar.activation(
-                    out=z_of[i][:, j, h * CH : (h + 1) * CH],
-                    in_=r_of[i][:, j, h * CH : (h + 1) * CH],
-                    func=ACT.Identity,
-                    scale=rstd_of[i][:, row : row + 1],
-                    bias=shift_of[i][:, row : row + 1],
-                )
+                if h % PACK == PACK - 1:
+                    nc.gpsimd.tensor_scalar(
+                        out=z_of[i][:, j, h * CH : (h + 1) * CH],
+                        in0=r_of[i][:, j, h * CH : (h + 1) * CH],
+                        scalar1=rstd_of[i][:, row : row + 1],
+                        scalar2=shift_of[i][:, row : row + 1],
+                        op0=ALU.mult,
+                        op1=ALU.add,
+                    )
+                else:
+                    nc.scalar.activation(
+                        out=z_of[i][:, j, h * CH : (h + 1) * CH],
+                        in_=r_of[i][:, j, h * CH : (h + 1) * CH],
+                        func=ACT.Identity,
+                        scale=rstd_of[i][:, row : row + 1],
+                        bias=shift_of[i][:, row : row + 1],
+                    )
 
         def transpose(i, h):
             zt = psum_t.tile([P, GROUP], F32)
@@ -243,13 +243,12 @@ def tile_retentivenetwork_pb_t_kernel(tc, ret, gamma, beta, Wo, bo, out):
             if exists(i + LOADS_AHEAD):
                 load(i + LOADS_AHEAD)
             if exists(i + 2):
-                halves(i + 2, range(0, TILES // 2))
+                moments(i + 2, range(0, TILES // 2))
             if exists(i + 1):
                 reciprocal(i + 1)
                 shift(i + 1)
             if exists(i + 2):
-                halves(i + 2, range(TILES // 2, TILES))
-                join_halves(i + 2)
+                moments(i + 2, range(TILES // 2, TILES))
             if i == -1:
                 gamma_beta_to_partitions()
             if exists(i):
@@ -264,6 +263,7 @@ def tile_retentivenetwork_pb_t_kernel(tc, ret, gamma, beta, Wo, bo, out):
                     if h < BANKS_T:
                         transpose(i + 1, h)
             if exists(i + 2):
+                variance(i + 2)
                 deviation(i + 2)
             if exists(i - 2):
                 add_bias_and_store(i - 2)

@@ -24,9 +24,10 @@ TILES = 4
 GROUP = TILES * P
 N_GROUPS = TOKENS // GROUP
 ROWS = TILES * HEADS
+GPSIMD_SHARE = {(h, j) for h in (1, 3, 5, 7) for j in range(4)}
 RUN = 4
 BANKS_T = 4
-LOADS_AHEAD = 4
+LOADS_AHEAD = 5
 
 FLOPS = 2 * TOKENS * D * E
 
@@ -39,16 +40,16 @@ def tile_retentivenetwork_pb_t_kernel(tc, ret, gamma, beta, Wo, bo, out):
     with ExitStack() as ctx:
         const = ctx.enter_context(tc.tile_pool(name="const", bufs=1))
         r_pool = ctx.enter_context(tc.tile_pool(name="r", bufs=LOADS_AHEAD + 1))
-        stat_pool = ctx.enter_context(tc.tile_pool(name="stat", bufs=3))
+        stat_pool = ctx.enter_context(tc.tile_pool(name="stat", bufs=4))
         z_pool = ctx.enter_context(tc.tile_pool(name="z", bufs=2))
         y_pool = ctx.enter_context(tc.tile_pool(name="y", bufs=3))
-        q_pool = ctx.enter_context(tc.tile_pool(name="q", bufs=2))
+        q_pool = ctx.enter_context(tc.tile_pool(name="q", bufs=4))
         o_pool = ctx.enter_context(tc.tile_pool(name="o", bufs=2))
         psum_t = ctx.enter_context(tc.psum_pool(name="psum_t", bufs=BANKS_T))
         psum_o = ctx.enter_context(tc.psum_pool(name="psum_o", bufs=TILES))
         ctx.enter_context(tc.manual_schedule())
 
-        r_of, st_of, minus_mean_of, var_eps_of, std_of, rstd_of, shift_of = {}, {}, {}, {}, {}, {}, {}
+        r_of, st_of, minus_mean_of, var_eps_of, rstd_of, shift_of = {}, {}, {}, {}, {}, {}
         z_of, zt_of, y_of, grouped_of, codes_of, scales_of, acc_of = {}, {}, {}, {}, {}, {}, {}
 
         def load(i):
@@ -62,7 +63,8 @@ def tile_retentivenetwork_pb_t_kernel(tc, ret, gamma, beta, Wo, bo, out):
             r_of[i] = r
 
         load(0)
-        load(1)
+        for i in range(1, LOADS_AHEAD - 3):
+            load(i)
         w_raw = const.tile([P, PASSES * PACK, E], BF16)
         nc.sync.dma_start(out=w_raw[:], in_=Wo.rearrange("(s p) n -> p s n", p=P))
 
@@ -78,7 +80,7 @@ def tile_retentivenetwork_pb_t_kernel(tc, ret, gamma, beta, Wo, bo, out):
 
         one = const.tile([P, 1], F32)
         nc.vector.memset(one[:], 1.0)
-        nc.scalar.activation(out=one[:], in_=one[:], func=ACT.Sqrt)
+        nc.scalar.activation(out=one[:], in_=one[:], func=ACT.Abs_reciprocal_sqrt)
 
         gb_col = const.tile([P, 2 * HEADS], F32)
 
@@ -133,14 +135,9 @@ def tile_retentivenetwork_pb_t_kernel(tc, ret, gamma, beta, Wo, bo, out):
             var_eps_of[i] = var_eps
             minus_mean_of[i] = minus_mean
 
-        def deviation(i):
-            std = stat_pool.tile([P, ROWS], F32)
-            nc.scalar.activation(out=std[:], in_=var_eps_of[i][:], func=ACT.Sqrt)
-            std_of[i] = std
-
-        def reciprocal(i):
+        def reciprocal_deviation(i):
             rstd = stat_pool.tile([P, ROWS], F32)
-            nc.vector.reciprocal(out=rstd[:], in_=std_of[i][:])
+            nc.scalar.activation(out=rstd[:], in_=var_eps_of[i][:], func=ACT.Abs_reciprocal_sqrt)
             rstd_of[i] = rstd
 
         def shift(i):
@@ -154,7 +151,7 @@ def tile_retentivenetwork_pb_t_kernel(tc, ret, gamma, beta, Wo, bo, out):
                 z_of[i] = z
             for j in range(TILES):
                 row = j * HEADS + h
-                if h % PACK == PACK - 1:
+                if (h, j) in GPSIMD_SHARE:
                     nc.gpsimd.tensor_scalar(
                         out=z_of[i][:, j, h * CH : (h + 1) * CH],
                         in0=r_of[i][:, j, h * CH : (h + 1) * CH],
@@ -190,10 +187,20 @@ def tile_retentivenetwork_pb_t_kernel(tc, ret, gamma, beta, Wo, bo, out):
                 bias=gb_col[:, HEADS + h : HEADS + h + 1],
             )
 
-        def group_words(i, g):
-            grouped = q_pool.tile([P, GROUP, PACK], BF16, align_bytes=64)
-            regroup(grouped[:], y_of[i][:, g * PACK : (g + 1) * PACK, :])
-            grouped_of[(i, g)] = grouped
+        def group_words(i, g, engine, tiles):
+            if (i, g) not in grouped_of:
+                grouped = q_pool.tile([P, GROUP, PACK], BF16, align_bytes=64)
+                grouped_of[(i, g)] = grouped
+            cols = slice(tiles[0] * P, (tiles[-1] + 1) * P)
+            dst = grouped_of[(i, g)][:, cols, :]
+            src = y_of[i][:, g * PACK : (g + 1) * PACK, cols]
+            if engine == "scalar":
+                nc.scalar.copy(
+                    out=dst.rearrange("p (c i) t -> p c t i", i=RUN),
+                    in_=src.rearrange("p t (c i) -> p c t i", i=RUN),
+                )
+            else:
+                regroup(dst, src)
 
         def quantise(i, g):
             if g == 0:
@@ -207,16 +214,14 @@ def tile_retentivenetwork_pb_t_kernel(tc, ret, gamma, beta, Wo, bo, out):
                 in_=grouped_of[(i, g)][:].rearrange("p w t -> p (w t)"),
             )
 
-        def project(i):
+        def project(i, steps):
             codes, scales = codes_of[i], scales_of[i]
-            accs = []
-            for j in range(TILES):
-                acc = psum_o.tile([P, E], F32)
-                accs.append(acc)
-            for g in range(PASSES):
-                for j in range(TILES):
+            for g, j in steps:
+                    if g == 0:
+                        acc = psum_o.tile([P, E], F32)
+                        acc_of[(i, j)] = acc
                     nc.tensor.matmul_mx(
-                        out=accs[j][:],
+                        out=acc_of[(i, j)][:],
                         lhsT=codes[:, g, j * P : (j + 1) * P].bitcast(FP8X4),
                         lhsT_scale=scales[:, g, j * P : (j + 1) * P],
                         rhs=w_codes[:, g, :].bitcast(FP8X4),
@@ -224,13 +229,12 @@ def tile_retentivenetwork_pb_t_kernel(tc, ret, gamma, beta, Wo, bo, out):
                         start=(g == 0),
                         stop=(g == PASSES - 1),
                     )
-            acc_of[i] = accs
 
         def add_bias_and_store(i):
             o = o_pool.tile([P, TILES, E], F32)
             rows = out_rows[i * GROUP : (i + 1) * GROUP, :].rearrange("(p j) e -> p j e", j=TILES)
             for j in range(TILES):
-                nc.vector.tensor_tensor(out=o[:, j, :], in0=acc_of[i][j][:], in1=bo_all[:], op=ALU.add)
+                nc.vector.tensor_tensor(out=o[:, j, :], in0=acc_of[(i, j)][:], in1=bo_all[:], op=ALU.add)
                 if i == N_GROUPS - 1:
                     nc.sync.dma_start(out=rows[:, j, :], in_=o[:, j, :])
             if i < N_GROUPS - 1:
@@ -239,39 +243,40 @@ def tile_retentivenetwork_pb_t_kernel(tc, ret, gamma, beta, Wo, bo, out):
         def exists(i):
             return 0 <= i < N_GROUPS
 
-        for i in range(-2, N_GROUPS + 2):
+        for i in range(-3, N_GROUPS + 2):
             if exists(i + LOADS_AHEAD):
                 load(i + LOADS_AHEAD)
             if exists(i + 2):
-                moments(i + 2, range(0, TILES // 2))
-            if exists(i + 1):
-                reciprocal(i + 1)
-                shift(i + 1)
-            if exists(i + 2):
-                moments(i + 2, range(TILES // 2, TILES))
-            if i == -1:
-                gamma_beta_to_partitions()
-            if exists(i):
-                for h in range(BANKS_T):
-                    affine(i, h)
-                    transpose(i, h + BANKS_T)
-                for h in range(BANKS_T, HEADS):
-                    affine(i, h)
-            if exists(i + 1):
-                for h in range(HEADS):
-                    normalise(i + 1, h)
-                    if h < BANKS_T:
-                        transpose(i + 1, h)
-            if exists(i + 2):
                 variance(i + 2)
-                deviation(i + 2)
+            if exists(i + 3):
+                moments(i + 3, range(0, TILES))
+            if i == -2:
+                gamma_beta_to_partitions()
+            mx = [(g, j) for g in range(PASSES) for j in range(TILES)] if exists(i - 2) else []
+            for h in range(HEADS):
+                if exists(i):
+                    affine(i, h)
+                    if h < BANKS_T:
+                        transpose(i, h + BANKS_T)
+                if mx and h >= 4:
+                    n = 8
+                    project(i - 2, mx[:n])
+                    mx = mx[n:]
+                if exists(i + 1):
+                    normalise(i + 1, h)
+                    if h >= BANKS_T:
+                        transpose(i + 1, h - BANKS_T)
+                if h == 3 and exists(i + 2):
+                    reciprocal_deviation(i + 2)
+            if exists(i + 2):
+                shift(i + 2)
+            if exists(i):
+                group_words(i, 0, "scalar", range(4))
             if exists(i - 2):
                 add_bias_and_store(i - 2)
             if i == 0:
                 quantise_weights()
             if exists(i - 1):
-                for g in range(PASSES):
-                    group_words(i - 1, g)
+                group_words(i - 1, 1, "vector", range(4))
                 for g in range(PASSES):
                     quantise(i - 1, g)
-                project(i - 1)

@@ -24,7 +24,6 @@ TILES = 4
 GROUP = TILES * P
 N_GROUPS = TOKENS // GROUP
 ROWS = TILES * HEADS
-GPSIMD_SHARE = {(h, j) for h in (1, 3, 5, 7) for j in range(4)}
 RUN = 4
 BANKS_T = 4
 LOADS_AHEAD = 5
@@ -43,13 +42,13 @@ def tile_retentivenetwork_pb_t_kernel(tc, ret, gamma, beta, Wo, bo, out):
         stat_pool = ctx.enter_context(tc.tile_pool(name="stat", bufs=4))
         z_pool = ctx.enter_context(tc.tile_pool(name="z", bufs=2))
         y_pool = ctx.enter_context(tc.tile_pool(name="y", bufs=3))
-        q_pool = ctx.enter_context(tc.tile_pool(name="q", bufs=4))
+        q_pool = ctx.enter_context(tc.tile_pool(name="q", bufs=2))
         o_pool = ctx.enter_context(tc.tile_pool(name="o", bufs=2))
         psum_t = ctx.enter_context(tc.psum_pool(name="psum_t", bufs=BANKS_T))
         psum_o = ctx.enter_context(tc.psum_pool(name="psum_o", bufs=TILES))
         ctx.enter_context(tc.manual_schedule())
 
-        r_of, st_of, minus_mean_of, var_eps_of, rstd_of, shift_of = {}, {}, {}, {}, {}, {}
+        r_of, st_of, minus_mean_of, rstd_of, shift_of = {}, {}, {}, {}, {}
         z_of, zt_of, y_of, grouped_of, codes_of, scales_of, acc_of = {}, {}, {}, {}, {}, {}, {}
 
         def load(i):
@@ -81,6 +80,8 @@ def tile_retentivenetwork_pb_t_kernel(tc, ret, gamma, beta, Wo, bo, out):
         one = const.tile([P, 1], F32)
         nc.vector.memset(one[:], 1.0)
         nc.scalar.activation(out=one[:], in_=one[:], func=ACT.Abs_reciprocal_sqrt)
+        eps_col = const.tile([P, 1], F32)
+        nc.vector.tensor_scalar(out=eps_col[:], in0=one[:], scalar1=0.0, scalar2=EPS, op0=ALU.mult, op1=ALU.add)
 
         gb_col = const.tile([P, 2 * HEADS], F32)
 
@@ -122,22 +123,18 @@ def tile_retentivenetwork_pb_t_kernel(tc, ret, gamma, beta, Wo, bo, out):
                         in_=r_of[i][:, j, 2 * pair * CH : (2 * pair + 2) * CH].rearrange("p (a c) -> p c a", a=2),
                     )
 
-        def variance(i):
-            st = st_of[i]
-            var_eps = stat_pool.tile([P, ROWS], F32)
+        def negate_mean(i):
             minus_mean = stat_pool.tile([P, ROWS], F32)
             nc.gpsimd.tensor_scalar(
-                out=var_eps[:], in0=st[:, :, 2], scalar1=1.0 / CH, scalar2=EPS, op0=ALU.mult, op1=ALU.add
+                out=minus_mean[:], in0=st_of[i][:, :, 1], scalar1=-1.0, scalar2=0.0, op0=ALU.mult, op1=ALU.add
             )
-            nc.gpsimd.tensor_scalar(
-                out=minus_mean[:], in0=st[:, :, 1], scalar1=-1.0, scalar2=0.0, op0=ALU.mult, op1=ALU.add
-            )
-            var_eps_of[i] = var_eps
             minus_mean_of[i] = minus_mean
 
         def reciprocal_deviation(i):
             rstd = stat_pool.tile([P, ROWS], F32)
-            nc.scalar.activation(out=rstd[:], in_=var_eps_of[i][:], func=ACT.Abs_reciprocal_sqrt)
+            nc.scalar.activation(
+                out=rstd[:], in_=st_of[i][:, :, 2], func=ACT.Abs_reciprocal_sqrt, scale=1.0 / CH, bias=eps_col[:]
+            )
             rstd_of[i] = rstd
 
         def shift(i):
@@ -151,22 +148,23 @@ def tile_retentivenetwork_pb_t_kernel(tc, ret, gamma, beta, Wo, bo, out):
                 z_of[i] = z
             for j in range(TILES):
                 row = j * HEADS + h
-                if (h, j) in GPSIMD_SHARE:
-                    nc.gpsimd.tensor_scalar(
-                        out=z_of[i][:, j, h * CH : (h + 1) * CH],
-                        in0=r_of[i][:, j, h * CH : (h + 1) * CH],
-                        scalar1=rstd_of[i][:, row : row + 1],
-                        scalar2=shift_of[i][:, row : row + 1],
-                        op0=ALU.mult,
-                        op1=ALU.add,
-                    )
-                else:
+                if norm_engine(i, h, j) == "scalar":
                     nc.scalar.activation(
                         out=z_of[i][:, j, h * CH : (h + 1) * CH],
                         in_=r_of[i][:, j, h * CH : (h + 1) * CH],
                         func=ACT.Identity,
                         scale=rstd_of[i][:, row : row + 1],
                         bias=shift_of[i][:, row : row + 1],
+                    )
+                else:
+                    engine = nc.vector if norm_engine(i, h, j) == "vector" else nc.gpsimd
+                    engine.tensor_scalar(
+                        out=z_of[i][:, j, h * CH : (h + 1) * CH],
+                        in0=r_of[i][:, j, h * CH : (h + 1) * CH],
+                        scalar1=rstd_of[i][:, row : row + 1],
+                        scalar2=shift_of[i][:, row : row + 1],
+                        op0=ALU.mult,
+                        op1=ALU.add,
                     )
 
         def transpose(i, h):
@@ -175,35 +173,44 @@ def tile_retentivenetwork_pb_t_kernel(tc, ret, gamma, beta, Wo, bo, out):
                 nc.tensor.transpose(zt[:, j * P : (j + 1) * P], z_of[i][:, j, h * CH : (h + 1) * CH], ident[:])
             zt_of[(i, h)] = zt
 
-        def affine(i, h):
-            if h == 0:
+        def affine(i, h, engine):
+            if i not in y_of:
                 y = y_pool.tile([P, HEADS, GROUP], BF16)
                 y_of[i] = y
-            nc.scalar.activation(
-                out=y_of[i][:, h, :],
-                in_=zt_of[(i, h)][:],
-                func=ACT.Identity,
-                scale=gb_col[:, h : h + 1],
-                bias=gb_col[:, HEADS + h : HEADS + h + 1],
-            )
+            if engine == "vector":
+                nc.vector.tensor_scalar(
+                    out=y_of[i][:, h, :],
+                    in0=zt_of[(i, h)][:],
+                    scalar1=gb_col[:, h : h + 1],
+                    scalar2=gb_col[:, HEADS + h : HEADS + h + 1],
+                    op0=ALU.mult,
+                    op1=ALU.add,
+                )
+            else:
+                nc.scalar.activation(
+                    out=y_of[i][:, h, :],
+                    in_=zt_of[(i, h)][:],
+                    func=ACT.Identity,
+                    scale=gb_col[:, h : h + 1],
+                    bias=gb_col[:, HEADS + h : HEADS + h + 1],
+                )
 
         def group_words(i, g, engine, tiles):
-            if (i, g) not in grouped_of:
-                grouped = q_pool.tile([P, GROUP, PACK], BF16, align_bytes=64)
-                grouped_of[(i, g)] = grouped
+            if i not in grouped_of:
+                grouped = q_pool.tile([P, PASSES, GROUP, PACK], BF16, align_bytes=64)
+                grouped_of[i] = grouped
             cols = slice(tiles[0] * P, (tiles[-1] + 1) * P)
-            dst = grouped_of[(i, g)][:, cols, :]
+            dst = grouped_of[i][:, g, cols, :]
             src = y_of[i][:, g * PACK : (g + 1) * PACK, cols]
-            if engine == "scalar":
-                nc.scalar.copy(
-                    out=dst.rearrange("p (c i) t -> p c t i", i=RUN),
-                    in_=src.rearrange("p t (c i) -> p c t i", i=RUN),
+            if engine == "gpsimd":
+                nc.gpsimd.tensor_scalar(
+                    out=dst, in0=src.rearrange("p t c -> p c t"), scalar1=1.0, scalar2=0.0, op0=ALU.mult, op1=ALU.add
                 )
             else:
                 regroup(dst, src)
 
         def quantise(i, g):
-            if g == 0:
+            if i not in codes_of:
                 codes = q_pool.tile([P, PASSES, GROUP], U32, align_bytes=64)
                 scales = q_pool.tile([P, PASSES, GROUP], U8, align_bytes=64)
                 codes_of[i] = codes
@@ -211,24 +218,24 @@ def tile_retentivenetwork_pb_t_kernel(tc, ret, gamma, beta, Wo, bo, out):
             nc.vector.quantize_mx(
                 out=codes_of[i][:, g, :].bitcast(FP8X4),
                 scales=scales_of[i][:, g, :],
-                in_=grouped_of[(i, g)][:].rearrange("p w t -> p (w t)"),
+                in_=grouped_of[i][:, g, :, :].rearrange("p w t -> p (w t)"),
             )
 
         def project(i, steps):
             codes, scales = codes_of[i], scales_of[i]
             for g, j in steps:
-                    if g == 0:
-                        acc = psum_o.tile([P, E], F32)
-                        acc_of[(i, j)] = acc
-                    nc.tensor.matmul_mx(
-                        out=acc_of[(i, j)][:],
-                        lhsT=codes[:, g, j * P : (j + 1) * P].bitcast(FP8X4),
-                        lhsT_scale=scales[:, g, j * P : (j + 1) * P],
-                        rhs=w_codes[:, g, :].bitcast(FP8X4),
-                        rhs_scale=w_scales[:, g, :],
-                        start=(g == 0),
-                        stop=(g == PASSES - 1),
-                    )
+                if g == 0:
+                    acc = psum_o.tile([P, E], F32)
+                    acc_of[(i, j)] = acc
+                nc.tensor.matmul_mx(
+                    out=acc_of[(i, j)][:],
+                    lhsT=codes[:, g, j * P : (j + 1) * P].bitcast(FP8X4),
+                    lhsT_scale=scales[:, g, j * P : (j + 1) * P],
+                    rhs=w_codes[:, g, :].bitcast(FP8X4),
+                    rhs_scale=w_scales[:, g, :],
+                    start=(g == 0),
+                    stop=(g == PASSES - 1),
+                )
 
         def add_bias_and_store(i):
             o = o_pool.tile([P, TILES, E], F32)
@@ -243,40 +250,46 @@ def tile_retentivenetwork_pb_t_kernel(tc, ret, gamma, beta, Wo, bo, out):
         def exists(i):
             return 0 <= i < N_GROUPS
 
-        for i in range(-3, N_GROUPS + 2):
+        def norm_engine(i, h, j):
+            return "scalar"
+
+        for i in range(-3, N_GROUPS + 1):
             if exists(i + LOADS_AHEAD):
                 load(i + LOADS_AHEAD)
             if exists(i + 2):
-                variance(i + 2)
-            if exists(i + 3):
-                moments(i + 3, range(0, TILES))
-            if i == -2:
-                gamma_beta_to_partitions()
-            mx = [(g, j) for g in range(PASSES) for j in range(TILES)] if exists(i - 2) else []
+                negate_mean(i + 2)
+            if i == 0:
+                quantise_weights()
+            if exists(i - 1):
+                for g in range(PASSES):
+                    quantise(i - 1, g)
+            mx = [(g, j) for g in range(PASSES) for j in range(TILES)] if exists(i - 1) else []
             for h in range(HEADS):
                 if exists(i):
-                    affine(i, h)
+                    affine(i, h, "vector" if h in ((3,) if i < N_GROUPS - 3 else (1, 3, 5, 7)) else "scalar")
                     if h < BANKS_T:
                         transpose(i, h + BANKS_T)
-                if mx and h >= 4:
+                if h == 3 and exists(i + 3):
+                    moments(i + 3, range(0, 4))
+                    if i == -2:
+                        gamma_beta_to_partitions()
+                if mx and h >= 2:
                     n = 8
-                    project(i - 2, mx[:n])
+                    project(i - 1, mx[:n])
                     mx = mx[n:]
                 if exists(i + 1):
                     normalise(i + 1, h)
                     if h >= BANKS_T:
                         transpose(i + 1, h - BANKS_T)
-                if h == 3 and exists(i + 2):
+                if h == (1 if i >= 0 else 7) and exists(i + 2):
                     reciprocal_deviation(i + 2)
-            if exists(i + 2):
-                shift(i + 2)
-            if exists(i):
-                group_words(i, 0, "scalar", range(4))
-            if exists(i - 2):
-                add_bias_and_store(i - 2)
-            if i == 0:
-                quantise_weights()
+                    shift(i + 2)
+                if exists(i):
+                    if h == BANKS_T - 1:
+                        for tiles in (range(0, 2), range(2, 4)):
+                            group_words(i, 0, "gpsimd", tiles)
+                    if h == HEADS - 1:
+                        for tiles in (range(0, 2), range(2, 4)):
+                            group_words(i, 1, "gpsimd", tiles)
             if exists(i - 1):
-                group_words(i - 1, 1, "vector", range(4))
-                for g in range(PASSES):
-                    quantise(i - 1, g)
+                add_bias_and_store(i - 1)

@@ -20,12 +20,13 @@ D = HEADS * CH
 E = 512
 EPS = 1e-5
 PASSES = D // (P * PACK)
-TILES = 4
-GROUP = TILES * P
-N_GROUPS = TOKENS // GROUP
-ROWS = TILES * HEADS
+MAX_TILES = 4
+TILES_OF = [4] * 14 + [2] * 4
+FIRST_TILE = [sum(TILES_OF[:i]) for i in range(len(TILES_OF))]
+N_GROUPS = len(TILES_OF)
 RUN = 4
-BANKS_T = 4
+BANKS_T = 5
+BANKS_O = 3
 LOADS_AHEAD = 5
 
 FLOPS = 2 * TOKENS * D * E
@@ -45,17 +46,21 @@ def tile_retentivenetwork_pb_t_kernel(tc, ret, gamma, beta, Wo, bo, out):
         q_pool = ctx.enter_context(tc.tile_pool(name="q", bufs=2))
         o_pool = ctx.enter_context(tc.tile_pool(name="o", bufs=2))
         psum_t = ctx.enter_context(tc.psum_pool(name="psum_t", bufs=BANKS_T))
-        psum_o = ctx.enter_context(tc.psum_pool(name="psum_o", bufs=TILES))
+        psum_o = ctx.enter_context(tc.psum_pool(name="psum_o", bufs=BANKS_O))
         ctx.enter_context(tc.manual_schedule())
 
         r_of, st_of, minus_mean_of, rstd_of, shift_of = {}, {}, {}, {}, {}
         z_of, zt_of, y_of, grouped_of, codes_of, scales_of, acc_of = {}, {}, {}, {}, {}, {}, {}
 
+        def token_rows(rows, i):
+            first, tiles = FIRST_TILE[i] * P, TILES_OF[i]
+            return rows[first : first + tiles * P, :].rearrange("(p j) k -> p j k", j=tiles)
+
         def load(i):
-            r = r_pool.tile([P, TILES, D], BF16)
-            rows = ret_rows[i * GROUP : (i + 1) * GROUP, :].rearrange("(p j) k -> p j k", j=TILES)
+            r = r_pool.tile([P, TILES_OF[i], D], BF16)
+            rows = token_rows(ret_rows, i)
             if i == 0:
-                for j in range(TILES):
+                for j in range(TILES_OF[i]):
                     nc.sync.dma_start(out=r[:, j, :], in_=rows[:, j, :])
             else:
                 nc.sync.dma_start(out=r[:], in_=rows)
@@ -88,7 +93,7 @@ def tile_retentivenetwork_pb_t_kernel(tc, ret, gamma, beta, Wo, bo, out):
         def gamma_beta_to_partitions():
             gb_f32 = const.tile([P, P], F32)
             nc.vector.tensor_copy(out=gb_f32[:], in_=gb_rows[:])
-            gb_t = psum_t.tile([P, GROUP], F32, tag="zt")
+            gb_t = psum_t.tile([P, MAX_TILES * P], F32, tag="zt")
             nc.tensor.transpose(gb_t[:, 0:P], gb_f32[:], ident[:])
             nc.vector.tensor_copy(out=gb_col[:], in_=gb_t[:, 0 : 2 * HEADS])
 
@@ -112,8 +117,8 @@ def tile_retentivenetwork_pb_t_kernel(tc, ret, gamma, beta, Wo, bo, out):
                 )
 
         def moments(i, tiles):
-            if tiles[0] == 0:
-                st = stat_pool.tile([P, ROWS, 3], F32)
+            if i not in st_of:
+                st = stat_pool.tile([P, TILES_OF[i] * HEADS, 3], F32)
                 st_of[i] = st
             for j in tiles:
                 for pair in range(HEADS // 2):
@@ -123,30 +128,26 @@ def tile_retentivenetwork_pb_t_kernel(tc, ret, gamma, beta, Wo, bo, out):
                         in_=r_of[i][:, j, 2 * pair * CH : (2 * pair + 2) * CH].rearrange("p (a c) -> p c a", a=2),
                     )
 
-        def negate_mean(i):
-            minus_mean = stat_pool.tile([P, ROWS], F32)
-            nc.gpsimd.tensor_scalar(
-                out=minus_mean[:], in0=st_of[i][:, :, 1], scalar1=-1.0, scalar2=0.0, op0=ALU.mult, op1=ALU.add
-            )
-            minus_mean_of[i] = minus_mean
-
         def reciprocal_deviation(i):
-            rstd = stat_pool.tile([P, ROWS], F32)
+            rstd = stat_pool.tile([P, TILES_OF[i] * HEADS], F32)
             nc.scalar.activation(
                 out=rstd[:], in_=st_of[i][:, :, 2], func=ACT.Abs_reciprocal_sqrt, scale=1.0 / CH, bias=eps_col[:]
             )
             rstd_of[i] = rstd
+            minus_mean = stat_pool.tile([P, TILES_OF[i] * HEADS], F32)
+            nc.scalar.activation(out=minus_mean[:], in_=st_of[i][:, :, 1], func=ACT.Copy, scale=-1.0)
+            minus_mean_of[i] = minus_mean
 
         def shift(i):
-            shift_tile = stat_pool.tile([P, ROWS], F32)
+            shift_tile = stat_pool.tile([P, TILES_OF[i] * HEADS], F32)
             nc.gpsimd.tensor_tensor(out=shift_tile[:], in0=minus_mean_of[i][:], in1=rstd_of[i][:], op=ALU.mult)
             shift_of[i] = shift_tile
 
         def normalise(i, h):
             if h == 0:
-                z = z_pool.tile([P, TILES, D], F32)
+                z = z_pool.tile([P, TILES_OF[i], D], F32)
                 z_of[i] = z
-            for j in range(TILES):
+            for j in range(TILES_OF[i]):
                 row = j * HEADS + h
                 if norm_engine(i, h, j) == "scalar":
                     nc.scalar.activation(
@@ -168,14 +169,14 @@ def tile_retentivenetwork_pb_t_kernel(tc, ret, gamma, beta, Wo, bo, out):
                     )
 
         def transpose(i, h):
-            zt = psum_t.tile([P, GROUP], F32)
-            for j in range(TILES):
+            zt = psum_t.tile([P, TILES_OF[i] * P], F32)
+            for j in range(TILES_OF[i]):
                 nc.tensor.transpose(zt[:, j * P : (j + 1) * P], z_of[i][:, j, h * CH : (h + 1) * CH], ident[:])
             zt_of[(i, h)] = zt
 
         def affine(i, h, engine):
             if i not in y_of:
-                y = y_pool.tile([P, HEADS, GROUP], BF16)
+                y = y_pool.tile([P, HEADS, TILES_OF[i] * P], BF16)
                 y_of[i] = y
             if engine == "vector":
                 nc.vector.tensor_scalar(
@@ -195,24 +196,29 @@ def tile_retentivenetwork_pb_t_kernel(tc, ret, gamma, beta, Wo, bo, out):
                     bias=gb_col[:, HEADS + h : HEADS + h + 1],
                 )
 
-        def group_words(i, g, engine, tiles):
+        def group_words(i, g, engine):
             if i not in grouped_of:
-                grouped = q_pool.tile([P, PASSES, GROUP, PACK], BF16, align_bytes=64)
+                grouped = q_pool.tile([P, PASSES, TILES_OF[i] * P, PACK], BF16, align_bytes=64)
                 grouped_of[i] = grouped
-            cols = slice(tiles[0] * P, (tiles[-1] + 1) * P)
-            dst = grouped_of[i][:, g, cols, :]
-            src = y_of[i][:, g * PACK : (g + 1) * PACK, cols]
             if engine == "gpsimd":
-                nc.gpsimd.tensor_scalar(
-                    out=dst, in0=src.rearrange("p t c -> p c t"), scalar1=1.0, scalar2=0.0, op0=ALU.mult, op1=ALU.add
-                )
+                step = 4
+                for first in range(0, TILES_OF[i], step):
+                    cols = slice(first * P, min(first + step, TILES_OF[i]) * P)
+                    nc.gpsimd.tensor_scalar(
+                        out=grouped_of[i][:, g, cols, :],
+                        in0=y_of[i][:, g * PACK : (g + 1) * PACK, cols].rearrange("p t c -> p c t"),
+                        scalar1=1.0,
+                        scalar2=0.0,
+                        op0=ALU.mult,
+                        op1=ALU.add,
+                    )
             else:
-                regroup(dst, src)
+                regroup(grouped_of[i][:, g, :, :], y_of[i][:, g * PACK : (g + 1) * PACK, :])
 
         def quantise(i, g):
             if i not in codes_of:
-                codes = q_pool.tile([P, PASSES, GROUP], U32, align_bytes=64)
-                scales = q_pool.tile([P, PASSES, GROUP], U8, align_bytes=64)
+                codes = q_pool.tile([P, PASSES, TILES_OF[i] * P], U32, align_bytes=64)
+                scales = q_pool.tile([P, PASSES, TILES_OF[i] * P], U8, align_bytes=64)
                 codes_of[i] = codes
                 scales_of[i] = scales
             nc.vector.quantize_mx(
@@ -221,26 +227,24 @@ def tile_retentivenetwork_pb_t_kernel(tc, ret, gamma, beta, Wo, bo, out):
                 in_=grouped_of[i][:, g, :, :].rearrange("p w t -> p (w t)"),
             )
 
-        def project(i, steps):
-            codes, scales = codes_of[i], scales_of[i]
-            for g, j in steps:
-                if g == 0:
-                    acc = psum_o.tile([P, E], F32)
-                    acc_of[(i, j)] = acc
-                nc.tensor.matmul_mx(
-                    out=acc_of[(i, j)][:],
-                    lhsT=codes[:, g, j * P : (j + 1) * P].bitcast(FP8X4),
-                    lhsT_scale=scales[:, g, j * P : (j + 1) * P],
-                    rhs=w_codes[:, g, :].bitcast(FP8X4),
-                    rhs_scale=w_scales[:, g, :],
-                    start=(g == 0),
-                    stop=(g == PASSES - 1),
-                )
+        def project(i, g, j):
+            if g == 0:
+                acc = psum_o.tile([P, E], F32)
+                acc_of[(i, j)] = acc
+            nc.tensor.matmul_mx(
+                out=acc_of[(i, j)][:],
+                lhsT=codes_of[i][:, g, j * P : (j + 1) * P].bitcast(FP8X4),
+                lhsT_scale=scales_of[i][:, g, j * P : (j + 1) * P],
+                rhs=w_codes[:, g, :].bitcast(FP8X4),
+                rhs_scale=w_scales[:, g, :],
+                start=(g == 0),
+                stop=(g == PASSES - 1),
+            )
 
         def add_bias_and_store(i):
-            o = o_pool.tile([P, TILES, E], F32)
-            rows = out_rows[i * GROUP : (i + 1) * GROUP, :].rearrange("(p j) e -> p j e", j=TILES)
-            for j in range(TILES):
+            o = o_pool.tile([P, TILES_OF[i], E], F32)
+            rows = token_rows(out_rows, i)
+            for j in range(TILES_OF[i]):
                 nc.vector.tensor_tensor(out=o[:, j, :], in0=acc_of[(i, j)][:], in1=bo_all[:], op=ALU.add)
                 if i == N_GROUPS - 1:
                     nc.sync.dma_start(out=rows[:, j, :], in_=o[:, j, :])
@@ -253,43 +257,47 @@ def tile_retentivenetwork_pb_t_kernel(tc, ret, gamma, beta, Wo, bo, out):
         def norm_engine(i, h, j):
             return "scalar"
 
+        def affine_engine(i, h):
+            return "vector" if h in (3, 5) else "scalar"
+
+        plan = {0: "q", 4: "d01", 5: "s", 6: "23g", 8: "b"}
+
         for i in range(-3, N_GROUPS + 1):
             if exists(i + LOADS_AHEAD):
                 load(i + LOADS_AHEAD)
-            if exists(i + 2):
-                negate_mean(i + 2)
             if i == 0:
                 quantise_weights()
-            if exists(i - 1):
-                for g in range(PASSES):
-                    quantise(i - 1, g)
-            mx = [(g, j) for g in range(PASSES) for j in range(TILES)] if exists(i - 1) else []
-            for h in range(HEADS):
-                if exists(i):
-                    affine(i, h, "vector" if h in ((3,) if i < N_GROUPS - 3 else (1, 3, 5, 7)) else "scalar")
-                    if h < BANKS_T:
-                        transpose(i, h + BANKS_T)
-                if h == 3 and exists(i + 3):
-                    moments(i + 3, range(0, 4))
-                    if i == -2:
+            mx = [(g, j) for j in range(TILES_OF[i - 1]) for g in range(PASSES)] if exists(i - 1) else []
+            mx0 = 3
+            for h in range(HEADS + 1):
+                for what in plan.get(h, ""):
+                    if what == "q" and exists(i - 1):
+                        for g in range(PASSES):
+                            quantise(i - 1, g)
+                    if what == "b" and exists(i - 1):
+                        add_bias_and_store(i - 1)
+                    if what in "0123" and exists(i + 3) and int(what) < TILES_OF[i + 3]:
+                        moments(i + 3, (int(what),))
+                    if what == "g" and i == -2:
                         gamma_beta_to_partitions()
-                if mx and h >= 2:
+                    if what == "s" and exists(i + 2):
+                        shift(i + 2)
+                    if what == "d" and exists(i + 2):
+                        reciprocal_deviation(i + 2)
+                if h == HEADS:
+                    break
+                if exists(i):
+                    affine(i, h, affine_engine(i, h))
+                    if h + BANKS_T < HEADS:
+                        transpose(i, h + BANKS_T)
+                if mx and h >= mx0:
                     n = 8
-                    project(i - 1, mx[:n])
+                    for g, j in mx[:n]:
+                        project(i - 1, g, j)
                     mx = mx[n:]
                 if exists(i + 1):
                     normalise(i + 1, h)
-                    if h >= BANKS_T:
-                        transpose(i + 1, h - BANKS_T)
-                if h == (1 if i >= 0 else 7) and exists(i + 2):
-                    reciprocal_deviation(i + 2)
-                    shift(i + 2)
-                if exists(i):
-                    if h == BANKS_T - 1:
-                        for tiles in (range(0, 2), range(2, 4)):
-                            group_words(i, 0, "gpsimd", tiles)
-                    if h == HEADS - 1:
-                        for tiles in (range(0, 2), range(2, 4)):
-                            group_words(i, 1, "gpsimd", tiles)
-            if exists(i - 1):
-                add_bias_and_store(i - 1)
+                    if h + BANKS_T >= HEADS:
+                        transpose(i + 1, h + BANKS_T - HEADS)
+                if exists(i) and h % PACK == PACK - 1:
+                    group_words(i, h // PACK, "vector" if i >= N_GROUPS - 0 else "gpsimd")

@@ -25,8 +25,8 @@ TILES_OF = [4] * 14 + [2] * 4
 FIRST_TILE = [sum(TILES_OF[:i]) for i in range(len(TILES_OF))]
 N_GROUPS = len(TILES_OF)
 RUN = 4
-BANKS_T = 5
-BANKS_O = 3
+BANKS_T = 4
+BANKS_O = 4
 LOADS_AHEAD = 5
 
 FLOPS = 2 * TOKENS * D * E
@@ -44,6 +44,7 @@ def tile_retentivenetwork_pb_t_kernel(tc, ret, gamma, beta, Wo, bo, out):
         z_pool = ctx.enter_context(tc.tile_pool(name="z", bufs=2))
         y_pool = ctx.enter_context(tc.tile_pool(name="y", bufs=3))
         q_pool = ctx.enter_context(tc.tile_pool(name="q", bufs=2))
+        g_pool = ctx.enter_context(tc.tile_pool(name="g", bufs=1))
         o_pool = ctx.enter_context(tc.tile_pool(name="o", bufs=2))
         psum_t = ctx.enter_context(tc.psum_pool(name="psum_t", bufs=BANKS_T))
         psum_o = ctx.enter_context(tc.psum_pool(name="psum_o", bufs=BANKS_O))
@@ -144,7 +145,7 @@ def tile_retentivenetwork_pb_t_kernel(tc, ret, gamma, beta, Wo, bo, out):
             shift_of[i] = shift_tile
 
         def normalise(i, h):
-            if h == 0:
+            if i not in z_of:
                 z = z_pool.tile([P, TILES_OF[i], D], F32)
                 z_of[i] = z
             for j in range(TILES_OF[i]):
@@ -197,15 +198,14 @@ def tile_retentivenetwork_pb_t_kernel(tc, ret, gamma, beta, Wo, bo, out):
                 )
 
         def group_words(i, g, engine):
-            if i not in grouped_of:
-                grouped = q_pool.tile([P, PASSES, TILES_OF[i] * P, PACK], BF16, align_bytes=64)
-                grouped_of[i] = grouped
+            grouped = g_pool.tile([P, TILES_OF[i] * P, PACK], BF16, align_bytes=64, tag="grouped%d" % g)
+            grouped_of[(i, g)] = grouped
             if engine == "gpsimd":
                 step = 4
                 for first in range(0, TILES_OF[i], step):
                     cols = slice(first * P, min(first + step, TILES_OF[i]) * P)
                     nc.gpsimd.tensor_scalar(
-                        out=grouped_of[i][:, g, cols, :],
+                        out=grouped_of[(i, g)][:, cols, :],
                         in0=y_of[i][:, g * PACK : (g + 1) * PACK, cols].rearrange("p t c -> p c t"),
                         scalar1=1.0,
                         scalar2=0.0,
@@ -213,7 +213,7 @@ def tile_retentivenetwork_pb_t_kernel(tc, ret, gamma, beta, Wo, bo, out):
                         op1=ALU.add,
                     )
             else:
-                regroup(grouped_of[i][:, g, :, :], y_of[i][:, g * PACK : (g + 1) * PACK, :])
+                regroup(grouped_of[(i, g)][:], y_of[i][:, g * PACK : (g + 1) * PACK, :])
 
         def quantise(i, g):
             if i not in codes_of:
@@ -224,7 +224,7 @@ def tile_retentivenetwork_pb_t_kernel(tc, ret, gamma, beta, Wo, bo, out):
             nc.vector.quantize_mx(
                 out=codes_of[i][:, g, :].bitcast(FP8X4),
                 scales=scales_of[i][:, g, :],
-                in_=grouped_of[i][:, g, :, :].rearrange("p w t -> p (w t)"),
+                in_=grouped_of[(i, g)][:].rearrange("p w t -> p (w t)"),
             )
 
         def project(i, g, j):
@@ -254,21 +254,26 @@ def tile_retentivenetwork_pb_t_kernel(tc, ret, gamma, beta, Wo, bo, out):
         def exists(i):
             return 0 <= i < N_GROUPS
 
+        def vector_heads(i):
+            return (3,)
+
+        plan = {0: "q0", 2: "1", 4: "d2", 5: "s", 6: "3g", 8: "b"}
+
         def norm_engine(i, h, j):
-            return "scalar"
-
-        def affine_engine(i, h):
-            return "vector" if h in (3, 5) else "scalar"
-
-        plan = {0: "q", 4: "d01", 5: "s", 6: "23g", 8: "b"}
+            return "gpsimd" if h == 2 else "scalar"
 
         for i in range(-3, N_GROUPS + 1):
             if exists(i + LOADS_AHEAD):
                 load(i + LOADS_AHEAD)
             if i == 0:
                 quantise_weights()
-            mx = [(g, j) for j in range(TILES_OF[i - 1]) for g in range(PASSES)] if exists(i - 1) else []
-            mx0 = 3
+            if exists(i):
+                for h in vector_heads(i):
+                    affine(i, h, "vector")
+            if exists(i + 1):
+                for h in ():
+                    normalise(i + 1, h)
+            mx = [(g, j) for g in range(PASSES) for j in range(TILES_OF[i - 1])] if exists(i - 1) else []
             for h in range(HEADS + 1):
                 for what in plan.get(h, ""):
                     if what == "q" and exists(i - 1):
@@ -287,17 +292,19 @@ def tile_retentivenetwork_pb_t_kernel(tc, ret, gamma, beta, Wo, bo, out):
                 if h == HEADS:
                     break
                 if exists(i):
-                    affine(i, h, affine_engine(i, h))
-                    if h + BANKS_T < HEADS:
+                    if h not in vector_heads(i):
+                        affine(i, h, "scalar")
+                    if h < BANKS_T:
                         transpose(i, h + BANKS_T)
-                if mx and h >= mx0:
+                if mx and h >= 3:
                     n = 8
                     for g, j in mx[:n]:
                         project(i - 1, g, j)
                     mx = mx[n:]
                 if exists(i + 1):
-                    normalise(i + 1, h)
-                    if h + BANKS_T >= HEADS:
-                        transpose(i + 1, h + BANKS_T - HEADS)
+                    if h not in ():
+                        normalise(i + 1, h)
+                    if h >= BANKS_T:
+                        transpose(i + 1, h - BANKS_T)
                 if exists(i) and h % PACK == PACK - 1:
-                    group_words(i, h // PACK, "vector" if i >= N_GROUPS - 0 else "gpsimd")
+                    group_words(i, h // PACK, "gpsimd")

@@ -21,7 +21,7 @@ E = 512
 EPS = 1e-5
 PASSES = D // (P * PACK)
 MAX_TILES = 4
-TILES_OF = [4] * 14 + [2] * 4
+TILES_OF = [4] * 15 + [2] * 2
 FIRST_TILE = [sum(TILES_OF[:i]) for i in range(len(TILES_OF))]
 N_GROUPS = len(TILES_OF)
 RUN = 4
@@ -107,14 +107,24 @@ def tile_retentivenetwork_pb_t_kernel(tc, ret, gamma, beta, Wo, bo, out):
                 in_=src.rearrange("p t (c i) -> p c t i", i=RUN),
             )
 
+        w_grouped = const.tile([P, PASSES, E, PACK], BF16, align_bytes=64)
+
+        def group_weights(g):
+            nc.gpsimd.tensor_scalar(
+                out=w_grouped[:, g, :, :],
+                in0=w_raw[:, g * PACK : (g + 1) * PACK, :].rearrange("p t n -> p n t"),
+                scalar1=1.0,
+                scalar2=0.0,
+                op0=ALU.mult,
+                op1=ALU.add,
+            )
+
         def quantise_weights():
             for g in range(PASSES):
-                w_grouped = const.tile([P, E, PACK], BF16, align_bytes=64, tag="w_grouped%d" % g)
-                regroup(w_grouped[:], w_raw[:, g * PACK : (g + 1) * PACK, :])
                 nc.vector.quantize_mx(
                     out=w_codes[:, g, :].bitcast(FP8X4),
                     scales=w_scales[:, g, :],
-                    in_=w_grouped[:].rearrange("p w t -> p (w t)"),
+                    in_=w_grouped[:, g, :, :].rearrange("p w t -> p (w t)"),
                 )
 
         def moments(i, tiles):
@@ -129,26 +139,36 @@ def tile_retentivenetwork_pb_t_kernel(tc, ret, gamma, beta, Wo, bo, out):
                         in_=r_of[i][:, j, 2 * pair * CH : (2 * pair + 2) * CH].rearrange("p (a c) -> p c a", a=2),
                     )
 
-        def reciprocal_deviation(i):
-            rstd = stat_pool.tile([P, TILES_OF[i] * HEADS], F32)
+        def reciprocal_deviation(i, tiles):
+            if i not in rstd_of:
+                rstd = stat_pool.tile([P, TILES_OF[i] * HEADS], F32)
+                minus_mean = stat_pool.tile([P, TILES_OF[i] * HEADS], F32)
+                rstd_of[i] = rstd
+                minus_mean_of[i] = minus_mean
+            rows = slice(tiles[0] * HEADS, (tiles[-1] + 1) * HEADS)
             nc.scalar.activation(
-                out=rstd[:], in_=st_of[i][:, :, 2], func=ACT.Abs_reciprocal_sqrt, scale=1.0 / CH, bias=eps_col[:]
+                out=rstd_of[i][:, rows],
+                in_=st_of[i][:, rows, 2],
+                func=ACT.Abs_reciprocal_sqrt,
+                scale=1.0 / CH,
+                bias=eps_col[:],
             )
-            rstd_of[i] = rstd
-            minus_mean = stat_pool.tile([P, TILES_OF[i] * HEADS], F32)
-            nc.scalar.activation(out=minus_mean[:], in_=st_of[i][:, :, 1], func=ACT.Copy, scale=-1.0)
-            minus_mean_of[i] = minus_mean
+            nc.scalar.activation(out=minus_mean_of[i][:, rows], in_=st_of[i][:, rows, 1], func=ACT.Copy, scale=-1.0)
 
-        def shift(i):
-            shift_tile = stat_pool.tile([P, TILES_OF[i] * HEADS], F32)
-            nc.gpsimd.tensor_tensor(out=shift_tile[:], in0=minus_mean_of[i][:], in1=rstd_of[i][:], op=ALU.mult)
-            shift_of[i] = shift_tile
+        def shift(i, tiles):
+            if i not in shift_of:
+                shift_tile = stat_pool.tile([P, TILES_OF[i] * HEADS], F32)
+                shift_of[i] = shift_tile
+            rows = slice(tiles[0] * HEADS, (tiles[-1] + 1) * HEADS)
+            nc.gpsimd.tensor_tensor(
+                out=shift_of[i][:, rows], in0=minus_mean_of[i][:, rows], in1=rstd_of[i][:, rows], op=ALU.mult
+            )
 
-        def normalise(i, h):
+        def normalise(i, h, tiles):
             if i not in z_of:
                 z = z_pool.tile([P, TILES_OF[i], D], F32)
                 z_of[i] = z
-            for j in range(TILES_OF[i]):
+            for j in tiles:
                 row = j * HEADS + h
                 if norm_engine(i, h, j) == "scalar":
                     nc.scalar.activation(
@@ -255,24 +275,33 @@ def tile_retentivenetwork_pb_t_kernel(tc, ret, gamma, beta, Wo, bo, out):
             return 0 <= i < N_GROUPS
 
         def vector_heads(i):
-            return (3,)
+            return () if i == 0 else (3,) if i % 2 else (2, 3)
 
         plan = {0: "q0", 2: "1", 4: "d2", 5: "s", 6: "3g", 8: "b"}
 
         def norm_engine(i, h, j):
-            return "gpsimd" if h == 2 else "scalar"
+            return "scalar"
 
         for i in range(-3, N_GROUPS + 1):
             if exists(i + LOADS_AHEAD):
                 load(i + LOADS_AHEAD)
-            if i == 0:
-                quantise_weights()
+            if i == -1:
+                for j in range(TILES_OF[0]):
+                    reciprocal_deviation(0, (j,))
+                    shift(0, (j,))
+                    for h in range(HEADS):
+                        normalise(0, h, (j,))
+            if i in (-1, 0) and True:
+                group_weights(i + 1)
             if exists(i):
                 for h in vector_heads(i):
                     affine(i, h, "vector")
             if exists(i + 1):
                 for h in ():
-                    normalise(i + 1, h)
+                    normalise(i + 1, h, range(TILES_OF[i + 1]))
+            if i == 0:
+                quantise_weights()
+            mx0 = 5
             mx = [(g, j) for g in range(PASSES) for j in range(TILES_OF[i - 1])] if exists(i - 1) else []
             for h in range(HEADS + 1):
                 for what in plan.get(h, ""):
@@ -283,12 +312,12 @@ def tile_retentivenetwork_pb_t_kernel(tc, ret, gamma, beta, Wo, bo, out):
                         add_bias_and_store(i - 1)
                     if what in "0123" and exists(i + 3) and int(what) < TILES_OF[i + 3]:
                         moments(i + 3, (int(what),))
-                    if what == "g" and i == -2:
+                    if what == "g" and i == -3:
                         gamma_beta_to_partitions()
-                    if what == "s" and exists(i + 2):
-                        shift(i + 2)
-                    if what == "d" and exists(i + 2):
-                        reciprocal_deviation(i + 2)
+                    if what == "s" and exists(i + 2) and i >= -1:
+                        shift(i + 2, range(TILES_OF[i + 2]))
+                    if what == "d" and exists(i + 2) and i >= -1:
+                        reciprocal_deviation(i + 2, range(TILES_OF[i + 2]))
                 if h == HEADS:
                     break
                 if exists(i):
@@ -296,15 +325,15 @@ def tile_retentivenetwork_pb_t_kernel(tc, ret, gamma, beta, Wo, bo, out):
                         affine(i, h, "scalar")
                     if h < BANKS_T:
                         transpose(i, h + BANKS_T)
-                if mx and h >= 3:
+                if mx and h >= mx0:
                     n = 8
                     for g, j in mx[:n]:
                         project(i - 1, g, j)
                     mx = mx[n:]
                 if exists(i + 1):
-                    if h not in ():
-                        normalise(i + 1, h)
+                    if i >= 0:
+                        normalise(i + 1, h, range(TILES_OF[i + 1]))
                     if h >= BANKS_T:
                         transpose(i + 1, h - BANKS_T)
                 if exists(i) and h % PACK == PACK - 1:
-                    group_words(i, h // PACK, "gpsimd")
+                    group_words(i, h // PACK, "vector" if i >= N_GROUPS - 3 else "gpsimd")

@@ -87,7 +87,9 @@ def tile_retentivenetwork_pb_t_kernel(tc, ret, gamma, beta, Wo, bo, out):
         nc.vector.memset(one[:], 1.0)
         nc.scalar.activation(out=one[:], in_=one[:], func=ACT.Abs_reciprocal_sqrt)
         eps_col = const.tile([P, 1], F32)
-        nc.vector.tensor_scalar(out=eps_col[:], in0=one[:], scalar1=0.0, scalar2=EPS, op0=ALU.mult, op1=ALU.add)
+        zero = const.tile([P, 1], F32)
+        nc.vector.memset(zero[:], 0.0)
+        nc.vector.tensor_scalar(out=eps_col[:], in0=zero[:], scalar1=1.0, scalar2=EPS, op0=ALU.mult, op1=ALU.add)
 
         gb_col = const.tile([P, 2 * HEADS], F32)
 
@@ -275,14 +277,16 @@ def tile_retentivenetwork_pb_t_kernel(tc, ret, gamma, beta, Wo, bo, out):
             return 0 <= i < N_GROUPS
 
         def vector_heads(i):
-            return () if i == 0 else (3,) if i % 2 else (2, 3)
+            return () if i == 0 else (2, 3) if i < N_GROUPS - 3 else (3,)
 
-        plan = {0: "q0", 2: "1", 4: "d2", 5: "s", 6: "3g", 8: "b"}
+        def by_vector(i, g):
+            return g == 1 and i == N_GROUPS - 1
 
         def norm_engine(i, h, j):
-            return "scalar"
+            return "vector" if i > 0 and h in () else "scalar"
 
         for i in range(-3, N_GROUPS + 1):
+            early = ()
             if exists(i + LOADS_AHEAD):
                 load(i + LOADS_AHEAD)
             if i == -1:
@@ -291,49 +295,45 @@ def tile_retentivenetwork_pb_t_kernel(tc, ret, gamma, beta, Wo, bo, out):
                     shift(0, (j,))
                     for h in range(HEADS):
                         normalise(0, h, (j,))
-            if i in (-1, 0) and True:
+            if i in (-1, 0):
                 group_weights(i + 1)
             if exists(i):
                 for h in vector_heads(i):
                     affine(i, h, "vector")
-            if exists(i + 1):
-                for h in ():
+            if i >= 0 and exists(i + 1):
+                for h in early:
                     normalise(i + 1, h, range(TILES_OF[i + 1]))
             if i == 0:
                 quantise_weights()
-            mx0 = 5
-            mx = [(g, j) for g in range(PASSES) for j in range(TILES_OF[i - 1])] if exists(i - 1) else []
-            for h in range(HEADS + 1):
-                for what in plan.get(h, ""):
-                    if what == "q" and exists(i - 1):
-                        for g in range(PASSES):
-                            quantise(i - 1, g)
-                    if what == "b" and exists(i - 1):
-                        add_bias_and_store(i - 1)
-                    if what in "0123" and exists(i + 3) and int(what) < TILES_OF[i + 3]:
-                        moments(i + 3, (int(what),))
-                    if what == "g" and i == -3:
-                        gamma_beta_to_partitions()
-                    if what == "s" and exists(i + 2) and i >= -1:
-                        shift(i + 2, range(TILES_OF[i + 2]))
-                    if what == "d" and exists(i + 2) and i >= -1:
-                        reciprocal_deviation(i + 2, range(TILES_OF[i + 2]))
-                if h == HEADS:
-                    break
+            if exists(i - 1):
+                for g in range(PASSES):
+                    if by_vector(i - 1, g):
+                        group_words(i - 1, g, "vector")
+                    quantise(i - 1, g)
+            if exists(i + 3):
+                moments(i + 3, range(TILES_OF[i + 3]))
+            if i == -3:
+                gamma_beta_to_partitions()
+            for h in range(HEADS):
+                if h == 4 and i >= -1 and exists(i + 2):
+                    reciprocal_deviation(i + 2, range(TILES_OF[i + 2]))
+                if h == 5 and i >= -1 and exists(i + 2):
+                    shift(i + 2, range(TILES_OF[i + 2]))
                 if exists(i):
                     if h not in vector_heads(i):
                         affine(i, h, "scalar")
                     if h < BANKS_T:
                         transpose(i, h + BANKS_T)
-                if mx and h >= mx0:
-                    n = 8
-                    for g, j in mx[:n]:
-                        project(i - 1, g, j)
-                    mx = mx[n:]
+                if h == 4 and exists(i - 1):
+                    for g in range(PASSES):
+                        for j in range(TILES_OF[i - 1]):
+                            project(i - 1, g, j)
                 if exists(i + 1):
-                    if i >= 0:
+                    if i >= 0 and h not in early:
                         normalise(i + 1, h, range(TILES_OF[i + 1]))
                     if h >= BANKS_T:
                         transpose(i + 1, h - BANKS_T)
-                if exists(i) and h % PACK == PACK - 1:
-                    group_words(i, h // PACK, "vector" if i >= N_GROUPS - 3 else "gpsimd")
+                if exists(i) and h % PACK == PACK - 1 and not by_vector(i, h // PACK):
+                    group_words(i, h // PACK, "gpsimd")
+            if exists(i - 1):
+                add_bias_and_store(i - 1)

@@ -113,8 +113,8 @@ def tile_retentivenetwork_pb_t_kernel(tc, ret, gamma, beta, Wo, bo, out):
 
         def group_weights(g):
             nc.gpsimd.tensor_scalar(
-                out=w_grouped[:, g, :, :],
-                in0=w_raw[:, g * PACK : (g + 1) * PACK, :].rearrange("p t n -> p n t"),
+                out=w_grouped[:, g, :, :].rearrange("p (c i) t -> p c t i", i=RUN),
+                in0=w_raw[:, g * PACK : (g + 1) * PACK, :].rearrange("p t (c i) -> p c t i", i=RUN),
                 scalar1=1.0,
                 scalar2=0.0,
                 op0=ALU.mult,
@@ -227,8 +227,8 @@ def tile_retentivenetwork_pb_t_kernel(tc, ret, gamma, beta, Wo, bo, out):
                 for first in range(0, TILES_OF[i], step):
                     cols = slice(first * P, min(first + step, TILES_OF[i]) * P)
                     nc.gpsimd.tensor_scalar(
-                        out=grouped_of[(i, g)][:, cols, :],
-                        in0=y_of[i][:, g * PACK : (g + 1) * PACK, cols].rearrange("p t c -> p c t"),
+                        out=grouped_of[(i, g)][:, cols, :].rearrange("p (c i) t -> p c t i", i=RUN),
+                        in0=y_of[i][:, g * PACK : (g + 1) * PACK, cols].rearrange("p t (c i) -> p c t i", i=RUN),
                         scalar1=1.0,
                         scalar2=0.0,
                         op0=ALU.mult,
@@ -283,7 +283,7 @@ def tile_retentivenetwork_pb_t_kernel(tc, ret, gamma, beta, Wo, bo, out):
             return g == 1 and i == N_GROUPS - 1
 
         def norm_engine(i, h, j):
-            return "vector" if i > 0 and h in () else "scalar"
+            return "gpsimd" if i > 0 and h == 5 and j == 0 else "scalar"
 
         for i in range(-3, N_GROUPS + 1):
             early = ()

@@ -283,7 +283,7 @@ def tile_retentivenetwork_pb_t_kernel(tc, ret, gamma, beta, Wo, bo, out):
             return g == 1 and i == N_GROUPS - 1
 
         def norm_engine(i, h, j):
-            return "gpsimd" if i > 0 and h == 5 and j == 0 else "scalar"
+            return "gpsimd" if i > 0 and h == 5 and j < 2 else "scalar"
 
         for i in range(-3, N_GROUPS + 1):
             early = ()

from contextlib import ExitStack

import concourse.mybir as mybir
from concourse.masks import make_identity

F32 = mybir.dt.float32
BF16 = mybir.dt.bfloat16
U32 = mybir.dt.uint32
U8 = mybir.dt.uint8
FP8X4 = mybir.dt.float8_e4m3fn_x4
ACT = mybir.ActivationFunctionType
ALU = mybir.AluOpType

P = 128
PACK = 4
TOKENS = 8 * 1024
HEADS = 8
CH = 128
D = HEADS * CH
E = 512
EPS = 1e-5
PASSES = D // (P * PACK)
MAX_TILES = 4
TILES_OF = [4] * 15 + [2] * 2
FIRST_TILE = [sum(TILES_OF[:i]) for i in range(len(TILES_OF))]
N_GROUPS = len(TILES_OF)
RUN = 4
BANKS_T = 4
BANKS_O = 4
LOADS_AHEAD = 5

FLOPS = 2 * TOKENS * D * E


def tile_retentivenetwork_pb_t_kernel(tc, ret, gamma, beta, Wo, bo, out):
    nc = tc.nc
    ret_rows = ret.rearrange("b t h c -> (b t) (h c)")
    out_rows = out.rearrange("b t e -> (b t) e")

    with ExitStack() as ctx:
        const = ctx.enter_context(tc.tile_pool(name="const", bufs=1))
        r_pool = ctx.enter_context(tc.tile_pool(name="r", bufs=LOADS_AHEAD + 1))
        stat_pool = ctx.enter_context(tc.tile_pool(name="stat", bufs=4))
        z_pool = ctx.enter_context(tc.tile_pool(name="z", bufs=2))
        y_pool = ctx.enter_context(tc.tile_pool(name="y", bufs=3))
        q_pool = ctx.enter_context(tc.tile_pool(name="q", bufs=2))
        g_pool = ctx.enter_context(tc.tile_pool(name="g", bufs=1))
        o_pool = ctx.enter_context(tc.tile_pool(name="o", bufs=2))
        psum_t = ctx.enter_context(tc.psum_pool(name="psum_t", bufs=BANKS_T))
        psum_o = ctx.enter_context(tc.psum_pool(name="psum_o", bufs=BANKS_O))
        ctx.enter_context(tc.manual_schedule())

        r_of, st_of, minus_mean_of, rstd_of, shift_of = {}, {}, {}, {}, {}
        z_of, zt_of, y_of, grouped_of, codes_of, scales_of, acc_of = {}, {}, {}, {}, {}, {}, {}

        def token_rows(rows, i):
            first, tiles = FIRST_TILE[i] * P, TILES_OF[i]
            return rows[first : first + tiles * P, :].rearrange("(p j) k -> p j k", j=tiles)

        def load(i):
            r = r_pool.tile([P, TILES_OF[i], D], BF16)
            rows = token_rows(ret_rows, i)
            if i == 0:
                for j in range(TILES_OF[i]):
                    nc.sync.dma_start(out=r[:, j, :], in_=rows[:, j, :])
            else:
                nc.sync.dma_start(out=r[:], in_=rows)
            r_of[i] = r

        load(0)
        for i in range(1, LOADS_AHEAD - 3):
            load(i)
        w_raw = const.tile([P, PASSES * PACK, E], BF16)
        nc.sync.dma_start(out=w_raw[:], in_=Wo.rearrange("(s p) n -> p s n", p=P))

        ident = const.tile([P, P], F32)
        make_identity(nc, ident[:])

        gb_rows = const.tile([P, P], BF16)
        nc.vector.memset(gb_rows[:], 0.0)
        nc.scalar.dma_start(out=gb_rows[0:HEADS, :], in_=gamma.rearrange("(h c) -> h c", c=CH))
        nc.scalar.dma_start(out=gb_rows[HEADS : 2 * HEADS, :], in_=beta.rearrange("(h c) -> h c", c=CH))
        bo_all = const.tile([P, E], BF16)
        nc.scalar.dma_start(out=bo_all[:], in_=bo.partition_broadcast(P))

        one = const.tile([P, 1], F32)
        nc.vector.memset(one[:], 1.0)
        nc.scalar.activation(out=one[:], in_=one[:], func=ACT.Abs_reciprocal_sqrt)
        eps_col = const.tile([P, 1], F32)
        zero = const.tile([P, 1], F32)
        nc.vector.memset(zero[:], 0.0)
        nc.vector.tensor_scalar(out=eps_col[:], in0=zero[:], scalar1=1.0, scalar2=EPS, op0=ALU.mult, op1=ALU.add)

        gb_col = const.tile([P, 2 * HEADS], F32)

        def gamma_beta_to_partitions():
            gb_f32 = const.tile([P, P], F32)
            nc.vector.tensor_copy(out=gb_f32[:], in_=gb_rows[:])
            gb_t = psum_t.tile([P, MAX_TILES * P], F32, tag="zt")
            nc.tensor.transpose(gb_t[:, 0:P], gb_f32[:], ident[:])
            nc.vector.tensor_copy(out=gb_col[:], in_=gb_t[:, 0 : 2 * HEADS])

        w_codes = const.tile([P, PASSES, E], U32, align_bytes=64)
        w_scales = const.tile([P, PASSES, E], U8, align_bytes=64)

        def regroup(dst, src):
            nc.vector.tensor_copy(
                out=dst.rearrange("p (c i) t -> p c t i", i=RUN),
                in_=src.rearrange("p t (c i) -> p c t i", i=RUN),
            )

        w_grouped = const.tile([P, PASSES, E, PACK], BF16, align_bytes=64)

        def group_weights(g):
            nc.gpsimd.tensor_scalar(
                out=w_grouped[:, g, :, :].rearrange("p (c i) t -> p c t i", i=RUN),
                in0=w_raw[:, g * PACK : (g + 1) * PACK, :].rearrange("p t (c i) -> p c t i", i=RUN),
                scalar1=1.0,
                scalar2=0.0,
                op0=ALU.mult,
                op1=ALU.add,
            )

        def quantise_weights():
            for g in range(PASSES):
                nc.vector.quantize_mx(
                    out=w_codes[:, g, :].bitcast(FP8X4),
                    scales=w_scales[:, g, :],
                    in_=w_grouped[:, g, :, :].rearrange("p w t -> p (w t)"),
                )

        def moments(i, tiles):
            if i not in st_of:
                st = stat_pool.tile([P, TILES_OF[i] * HEADS, 3], F32)
                st_of[i] = st
            for j in tiles:
                for pair in range(HEADS // 2):
                    row = j * HEADS + 2 * pair
                    nc.vector.bn_stats(
                        out=st_of[i][:, row : row + 2, :].rearrange("p a s -> p (a s)"),
                        in_=r_of[i][:, j, 2 * pair * CH : (2 * pair + 2) * CH].rearrange("p (a c) -> p c a", a=2),
                    )

        def reciprocal_deviation(i, tiles):
            if i not in rstd_of:
                rstd = stat_pool.tile([P, TILES_OF[i] * HEADS], F32)
                minus_mean = stat_pool.tile([P, TILES_OF[i] * HEADS], F32)
                rstd_of[i] = rstd
                minus_mean_of[i] = minus_mean
            rows = slice(tiles[0] * HEADS, (tiles[-1] + 1) * HEADS)
            nc.scalar.activation(
                out=rstd_of[i][:, rows],
                in_=st_of[i][:, rows, 2],
                func=ACT.Abs_reciprocal_sqrt,
                scale=1.0 / CH,
                bias=eps_col[:],
            )
            nc.scalar.activation(out=minus_mean_of[i][:, rows], in_=st_of[i][:, rows, 1], func=ACT.Copy, scale=-1.0)

        def shift(i, tiles):
            if i not in shift_of:
                shift_tile = stat_pool.tile([P, TILES_OF[i] * HEADS], F32)
                shift_of[i] = shift_tile
            rows = slice(tiles[0] * HEADS, (tiles[-1] + 1) * HEADS)
            nc.gpsimd.tensor_tensor(
                out=shift_of[i][:, rows], in0=minus_mean_of[i][:, rows], in1=rstd_of[i][:, rows], op=ALU.mult
            )

        def normalise(i, h, tiles):
            if i not in z_of:
                z = z_pool.tile([P, TILES_OF[i], D], F32)
                z_of[i] = z
            for j in tiles:
                row = j * HEADS + h
                if norm_engine(i, h, j) == "scalar":
                    nc.scalar.activation(
                        out=z_of[i][:, j, h * CH : (h + 1) * CH],
                        in_=r_of[i][:, j, h * CH : (h + 1) * CH],
                        func=ACT.Identity,
                        scale=rstd_of[i][:, row : row + 1],
                        bias=shift_of[i][:, row : row + 1],
                    )
                else:
                    engine = nc.vector if norm_engine(i, h, j) == "vector" else nc.gpsimd
                    engine.tensor_scalar(
                        out=z_of[i][:, j, h * CH : (h + 1) * CH],
                        in0=r_of[i][:, j, h * CH : (h + 1) * CH],
                        scalar1=rstd_of[i][:, row : row + 1],
                        scalar2=shift_of[i][:, row : row + 1],
                        op0=ALU.mult,
                        op1=ALU.add,
                    )

        def transpose(i, h):
            zt = psum_t.tile([P, TILES_OF[i] * P], F32)
            for j in range(TILES_OF[i]):
                nc.tensor.transpose(zt[:, j * P : (j + 1) * P], z_of[i][:, j, h * CH : (h + 1) * CH], ident[:])
            zt_of[(i, h)] = zt

        def affine(i, h, engine):
            if i not in y_of:
                y = y_pool.tile([P, HEADS, TILES_OF[i] * P], BF16)
                y_of[i] = y
            if engine == "vector":
                nc.vector.tensor_scalar(
                    out=y_of[i][:, h, :],
                    in0=zt_of[(i, h)][:],
                    scalar1=gb_col[:, h : h + 1],
                    scalar2=gb_col[:, HEADS + h : HEADS + h + 1],
                    op0=ALU.mult,
                    op1=ALU.add,
                )
            else:
                nc.scalar.activation(
                    out=y_of[i][:, h, :],
                    in_=zt_of[(i, h)][:],
                    func=ACT.Identity,
                    scale=gb_col[:, h : h + 1],
                    bias=gb_col[:, HEADS + h : HEADS + h + 1],
                )

        def group_words(i, g, engine):
            grouped = g_pool.tile([P, TILES_OF[i] * P, PACK], BF16, align_bytes=64, tag="grouped%d" % g)
            grouped_of[(i, g)] = grouped
            if engine == "gpsimd":
                step = 4
                for first in range(0, TILES_OF[i], step):
                    cols = slice(first * P, min(first + step, TILES_OF[i]) * P)
                    nc.gpsimd.tensor_scalar(
                        out=grouped_of[(i, g)][:, cols, :].rearrange("p (c i) t -> p c t i", i=RUN),
                        in0=y_of[i][:, g * PACK : (g + 1) * PACK, cols].rearrange("p t (c i) -> p c t i", i=RUN),
                        scalar1=1.0,
                        scalar2=0.0,
                        op0=ALU.mult,
                        op1=ALU.add,
                    )
            else:
                regroup(grouped_of[(i, g)][:], y_of[i][:, g * PACK : (g + 1) * PACK, :])

        def quantise(i, g):
            if i not in codes_of:
                codes = q_pool.tile([P, PASSES, TILES_OF[i] * P], U32, align_bytes=64)
                scales = q_pool.tile([P, PASSES, TILES_OF[i] * P], U8, align_bytes=64)
                codes_of[i] = codes
                scales_of[i] = scales
            nc.vector.quantize_mx(
                out=codes_of[i][:, g, :].bitcast(FP8X4),
                scales=scales_of[i][:, g, :],
                in_=grouped_of[(i, g)][:].rearrange("p w t -> p (w t)"),
            )

        def project(i, g, j):
            if g == 0:
                acc = psum_o.tile([P, E], F32)
                acc_of[(i, j)] = acc
            nc.tensor.matmul_mx(
                out=acc_of[(i, j)][:],
                lhsT=codes_of[i][:, g, j * P : (j + 1) * P].bitcast(FP8X4),
                lhsT_scale=scales_of[i][:, g, j * P : (j + 1) * P],
                rhs=w_codes[:, g, :].bitcast(FP8X4),
                rhs_scale=w_scales[:, g, :],
                start=(g == 0),
                stop=(g == PASSES - 1),
            )

        def add_bias_and_store(i):
            o = o_pool.tile([P, TILES_OF[i], E], F32)
            rows = token_rows(out_rows, i)
            for j in range(TILES_OF[i]):
                nc.vector.tensor_tensor(out=o[:, j, :], in0=acc_of[(i, j)][:], in1=bo_all[:], op=ALU.add)
                if i == N_GROUPS - 1:
                    nc.sync.dma_start(out=rows[:, j, :], in_=o[:, j, :])
            if i < N_GROUPS - 1:
                nc.sync.dma_start(out=rows, in_=o[:])

        def exists(i):
            return 0 <= i < N_GROUPS

        def vector_heads(i):
            return () if i == 0 else (2, 3) if i < N_GROUPS - 3 else (3,)

        def by_vector(i, g):
            return g == 1 and i == N_GROUPS - 1

        def norm_engine(i, h, j):
            return "gpsimd" if i > 0 and h == 5 and j < 2 else "scalar"

        for i in range(-3, N_GROUPS + 1):
            early = ()
            if exists(i + LOADS_AHEAD):
                load(i + LOADS_AHEAD)
            if i == -1:
                for j in range(TILES_OF[0]):
                    reciprocal_deviation(0, (j,))
                    shift(0, (j,))
                    for h in range(HEADS):
                        normalise(0, h, (j,))
            if i in (-1, 0):
                group_weights(i + 1)
            if exists(i):
                for h in vector_heads(i):
                    affine(i, h, "vector")
            if i >= 0 and exists(i + 1):
                for h in early:
                    normalise(i + 1, h, range(TILES_OF[i + 1]))
            if i == 0:
                quantise_weights()
            if exists(i - 1):
                for g in range(PASSES):
                    if by_vector(i - 1, g):
                        group_words(i - 1, g, "vector")
                    quantise(i - 1, g)
            if exists(i + 3):
                moments(i + 3, range(TILES_OF[i + 3]))
            if i == -3:
                gamma_beta_to_partitions()
            for h in range(HEADS):
                if h == 4 and i >= -1 and exists(i + 2):
                    reciprocal_deviation(i + 2, range(TILES_OF[i + 2]))
                if h == 5 and i >= -1 and exists(i + 2):
                    shift(i + 2, range(TILES_OF[i + 2]))
                if exists(i):
                    if h not in vector_heads(i):
                        affine(i, h, "scalar")
                    if h < BANKS_T:
                        transpose(i, h + BANKS_T)
                if h == 4 and exists(i - 1):
                    for g in range(PASSES):
                        for j in range(TILES_OF[i - 1]):
                            project(i - 1, g, j)
                if exists(i + 1):
                    if i >= 0 and h not in early:
                        normalise(i + 1, h, range(TILES_OF[i + 1]))
                    if h >= BANKS_T:
                        transpose(i + 1, h - BANKS_T)
                if exists(i) and h % PACK == PACK - 1 and not by_vector(i, h // PACK):
                    group_words(i, h // PACK, "gpsimd")
            if exists(i - 1):
                add_bias_and_store(i - 1)
